import numpy as np
import ml_dtypes


def mxq(x, axis, fmt="e4m3"):
    dtype, down = {"e4m3": (ml_dtypes.float8_e4m3fn, 7), "e5m2": (ml_dtypes.float8_e5m2, 14)}[fmt]
    v = np.moveaxis(np.asarray(x, np.float32).astype(ml_dtypes.bfloat16).astype(np.float64), axis, -1)
    blocks = v.reshape(v.shape[:-1] + (-1, 32))
    amax = np.abs(blocks).max(-1, keepdims=True)
    byte = np.maximum(np.where(amax > 0, np.frexp(amax)[1] - 1 + 127, 0) - down, 1)
    scale = np.exp2(byte - 127.0)
    codes = (blocks / scale).astype(np.float32).astype(dtype).astype(np.float64)
    return np.moveaxis((codes * scale).reshape(v.shape), -1, axis)


WIDE = False


def mx_kscale(k):
    if not WIDE:
        return np.ones(k)
    levels = np.array([10, -10, 5, -5, 0])
    a = np.random.permutation(np.resize(levels, k // 512 * 4)).reshape(k // 512, 4)
    idx = np.arange(k)
    return np.exp2(a[idx // 512, idx % 128 // 32])


BF16 = ml_dtypes.bfloat16


def bf(x):
    return np.asarray(x, np.float32).astype(BF16)


def f64(x):
    return np.asarray(x).astype(np.float64)


E2M1 = np.array([0.0, 0.5, 1.0, 1.5, 2.0, 3.0, 4.0, 6.0, -0.0, -0.5, -1.0, -1.5, -2.0, -3.0, -4.0, -6.0])


def pack_weight(w, fmt):
    k, n = w.shape
    w = f64(bf(w)).reshape(k // 32, 32, n)
    amax = np.abs(w).max(1)
    if fmt == "e4m3":
        byte = np.frexp(amax)[1] - 1 + 127 - 7
    else:
        mant, ex = np.frexp(amax / 6.0)
        byte = np.where(mant > 0.5, ex, ex - 1) + 127
    byte = np.clip(np.where(amax > 0, byte, 1), 1, 254)
    scaled = (w * np.exp2(127.0 - byte)[:, None, :]).reshape(k, n).astype(np.float32)
    by_word = np.ascontiguousarray(scaled.reshape(k // 512, 128, 4, n).transpose(0, 1, 3, 2))
    if fmt == "e4m3":
        words = by_word.astype(ml_dtypes.float8_e4m3fn).view(np.uint8)
    else:
        c = by_word.astype(ml_dtypes.float4_e2m1fn).view(np.uint8) & 0xF
        words = c[..., 0::2] | (c[..., 1::2] << 4)
    return np.ascontiguousarray(words), np.ascontiguousarray(byte.astype(np.uint8).reshape(k // 512, 16, n))


def unpack_weight(words, scales, fmt):
    g, p, n, _ = words.shape
    if fmt == "e4m3":
        vals = np.ascontiguousarray(words).view(ml_dtypes.float8_e4m3fn).astype(np.float64)
    else:
        nib = np.empty((g, p, n, 4), np.uint8)
        nib[..., 0::2] = words & 0xF
        nib[..., 1::2] = words >> 4
        vals = E2M1[nib]
    vals = vals * np.repeat(np.exp2(scales.astype(np.float64) - 127.0), 8, axis=1)[..., None]
    return vals.transpose(0, 1, 3, 2).reshape(g * 512, n)


B, S, D_MODEL, D_POS, H, D_FF = 512, 2, 1024, 512, 4, 2048
DPP = D_POS // H
DPH = D_MODEL // H


def setup_inputs():
    s = mx_kscale(D_MODEL)
    gq = np.exp2(np.random.uniform(-1.0, 1.0, (S, H, B, 1)))
    gk = np.exp2(np.random.uniform(-1.0, 1.0, (S, H, B, 1)))
    q_pos = bf(np.random.standard_normal((S, H, B, DPP)) * gq * 3.0 / np.sqrt(DPP))
    k_pos = bf(np.random.standard_normal((S, H, B, DPP)) * gk * 3.0 / np.sqrt(DPP))
    x_grp = bf(np.random.standard_normal((S, B, D_MODEL)) * s)
    wv = np.random.standard_normal((D_MODEL, D_MODEL)) * 0.5 / np.sqrt(D_MODEL) / s
    words, scales = pack_weight(np.ascontiguousarray(wv.T), "e4m3")
    bv = bf(np.random.standard_normal(D_MODEL) * 10.0 / B)
    return {"q_pos": q_pos,
            "k_pos": k_pos,
            "x_grp": x_grp,
            "Wv_words": words,
            "Wv_scales": scales,
            "bv": bv}


def reference(q_pos, k_pos, x_grp, Wv_words, Wv_scales, bv):
    v = (mxq(f64(x_grp), 2, "e4m3") @ unpack_weight(Wv_words, Wv_scales, "e4m3")) + f64(bv)
    v = v.reshape(S, B, H, DPH).transpose(0, 2, 1, 3)
    q2 = np.sum(f64(q_pos) * f64(q_pos), axis=-1)
    k2 = np.sum(f64(k_pos) * f64(k_pos), axis=-1)
    d2 = q2[..., :, None] + k2[..., None, :] - 2.0 * (f64(q_pos) @ f64(k_pos).transpose(0, 1, 3, 2))
    dist = np.sqrt(np.maximum(d2, 1e-12)) + 1.0
    scores = 1.0 / dist
    causal = np.triu(np.ones((B, B), bool), k=1)
    scores = np.where(causal, 0.0, scores)
    o = mxq(scores, 3, "e4m3") @ mxq(v, 2, "e4m3")
    return o.transpose(0, 2, 1, 3).reshape(S, B, D_MODEL)

@@ -1,0 +1,295 @@
+import concourse.mybir as mybir
+from concourse.masks import make_identity
+
+FLOPS = 2 * 1024 * 1024 * 1024 + 8 * 2 * 512 * 512 * (128 + 256)
+
+F32 = mybir.dt.float32
+BF16 = mybir.dt.bfloat16
+I32 = mybir.dt.int32
+U32 = mybir.dt.uint32
+U8 = mybir.dt.uint8
+FP8X4 = mybir.dt.float8_e4m3fn_x4
+ACT = mybir.ActivationFunctionType
+ALU = mybir.AluOpType
+
+P = 128
+PACK = 4
+GROUPS = 2
+HEADS = 4
+TOKENS = 512
+TILES = TOKENS // P
+D_MODEL = 1024
+PASSES = D_MODEL // (P * PACK)
+D_HEAD = D_MODEL // HEADS
+CHUNKS = D_MODEL // P
+UNITS = HEADS * TILES
+PIECES = 3
+D2_FLOOR = 1e-12
+MASKED_LOG = 1e30
+
+
+def tile_networklayer_pb_kernel(tc, q_pos, k_pos, x_grp, Wv_words, Wv_scales, bv, out):
+    nc = tc.nc
+    with tc.tile_pool(name="keep", bufs=1) as keep, tc.tile_pool(name="ring", bufs=3) as ring, tc.tile_pool(
+        name="logs", bufs=GROUPS * HEADS
+    ) as logs, tc.psum_pool(name="project", bufs=3) as psum_project:
+        ident_bf = keep.tile([P, P], BF16)
+        ident_f32 = keep.tile([P, P], F32)
+        selector = keep.tile([P, UNITS], BF16)
+        bias_rows = keep.tile([P, D_MODEL], BF16)
+        q_rows = [keep.tile([P, UNITS, P], BF16, name="q_rows%d" % s) for s in range(GROUPS)]
+        k_rows = [keep.tile([P, UNITS, P], BF16, name="k_rows%d" % s) for s in range(GROUPS)]
+        x_rows = [keep.tile([P, TILES, D_MODEL], BF16, name="x_rows%d" % s) for s in range(GROUPS)]
+        w_words = keep.tile([P, PASSES, D_MODEL], U32, align_bytes=64)
+        w_scales = keep.tile([P, PASSES, D_MODEL], U8, align_bytes=64)
+        x_codes = keep.tile([P, GROUPS * TILES, PASSES * P], U32, align_bytes=64)
+        x_scales = keep.tile([P, GROUPS * TILES, PASSES * P], U8, align_bytes=64)
+        v_grouped = [keep.tile([P, D_MODEL, PACK], BF16, name="v_grouped%d" % s, align_bytes=64) for s in range(GROUPS)]
+        v_codes = keep.tile([P, GROUPS, D_MODEL], U32, align_bytes=64)
+        v_scales = keep.tile([P, GROUPS, D_MODEL], U8, align_bytes=64)
+        qk_cols = keep.tile([P, GROUPS * HEADS, 2, TOKENS], BF16)
+        squares = keep.tile([P, UNITS, P], BF16)
+        q2 = [keep.tile([P, UNITS], F32, name="q2_%d" % s) for s in range(GROUPS)]
+        k2 = [keep.tile([P, UNITS], F32, name="k2_%d" % s) for s in range(GROUPS)]
+        minus_half_k2 = [keep.tile([P, UNITS], F32, name="minus_half_k2_%d" % s) for s in range(GROUPS)]
+        q2_rest = [keep.tile([P, 2, UNITS], F32, name="q2_rest%d" % s) for s in range(GROUPS)]
+        q2_pieces = [keep.tile([P, P], BF16, name="q2_pieces%d" % s) for s in range(GROUPS)]
+        q2_piece_rows = [keep.tile([P, P], BF16, name="q2_piece_rows%d" % s) for s in range(GROUPS)]
+        w_grouped = [keep.tile([P, TOKENS, PACK], BF16, name="w_grouped%d" % n, align_bytes=64) for n in range(3)]
+
+        nc.vector.memset(w_scales[:].rearrange("p g n -> p (g n)").bitcast(I32), 0)
+        make_identity(nc, ident_bf[:])
+        make_identity(nc, ident_f32[:])
+        for s in range(GROUPS):
+            nc.vector.memset(q2_pieces[s][:].bitcast(I32), 0)
+        for tile in w_grouped:
+            nc.vector.memset(tile[:].rearrange("p b t -> p (b t)").bitcast(I32), 0)
+        nc.vector.tensor_tensor(out=selector[:], in0=ident_bf[:, 0:UNITS], in1=ident_bf[:, UNITS : 2 * UNITS], op=ALU.add)
+        nc.vector.tensor_tensor(out=selector[:], in0=selector[:], in1=ident_bf[:, 2 * UNITS : 3 * UNITS], op=ALU.add)
+        nc.vector.tensor_scalar(out=selector[:], in0=selector[:], scalar1=-0.5, scalar2=None, op0=ALU.mult)
+
+        def load_rows(rows, source):
+            nc.sync.dma_start(out=rows[:], in_=source.rearrange("h (i p) d -> p (h i) d", p=P))
+
+        def load_x(s):
+            for half in range(2):
+                tiles = slice(2 * half, 2 * half + 2)
+                nc.sync.dma_start(out=x_rows[s][:, tiles, :], in_=x_grp[s].rearrange("(t p) k -> p t k", p=P)[:, tiles, :])
+
+        nc.scalar.dma_start(out=bias_rows[:], in_=bv.partition_broadcast(P))
+        load_rows(q_rows[0], q_pos[0])
+        load_rows(k_rows[0], k_pos[0])
+        load_x(0)
+        for quadrant in range(4):
+            nc.sync.dma_start(
+                out=w_scales[32 * quadrant : 32 * quadrant + 4, :, :].bitcast(I32),
+                in_=Wv_scales[:, 4 * quadrant : 4 * quadrant + 4, :].rearrange("g r n -> r g n").bitcast(I32),
+            )
+        for g in range(PASSES):
+            nc.sync.dma_start(out=w_words[:, g, :].bitcast(I32), in_=Wv_words[g].rearrange("p n t -> p (n t)").bitcast(I32))
+        load_rows(q_rows[1], q_pos[1])
+        load_rows(k_rows[1], k_pos[1])
+        load_x(1)
+
+        def regroup_x(psum_turn, s, t):
+            words = x_rows[s][:, t, :].bitcast(F32)
+            turned = psum_turn.tile([P, PASSES, 2, P], F32, tag="turned")
+            for g in range(PASSES):
+                for u in range(2):
+                    nc.tensor.transpose(turned[:, g, u, :], words[:, 256 * g + u : 256 * (g + 1) : 2], ident_f32[:])
+            x_grouped = ring.tile([P, PASSES, P, PACK], BF16, align_bytes=64)
+            nc.vector.tensor_copy(out=x_grouped[:].bitcast(F32), in_=turned[:].rearrange("p g u m -> p g m u"))
+            return x_grouped
+
+        def quantise_x(s, t, x_grouped):
+            nc.vector.quantize_mx(
+                out=x_codes[:, TILES * s + t, :].bitcast(FP8X4),
+                scales=x_scales[:, TILES * s + t, :],
+                in_=x_grouped[:].rearrange("p g m j -> p (g m j)"),
+            )
+
+        def quantise_x_group(psum_turn, s):
+            waiting = None
+            for t in range(TILES):
+                x_grouped = regroup_x(psum_turn, s, t)
+                if waiting is not None:
+                    quantise_x(s, t - 1, waiting)
+                waiting = x_grouped
+            quantise_x(s, TILES - 1, waiting)
+
+        def project_chunk(s, j):
+            cols = slice(P * j, P * (j + 1))
+            bank = psum_project.tile([P, TILES, P], F32, tag="bank")
+            for t in range(TILES):
+                for g in range(PASSES):
+                    tokens = slice(P * g, P * (g + 1))
+                    nc.tensor.matmul_mx(
+                        out=bank[:, t, :],
+                        lhsT=x_codes[:, TILES * s + t, tokens].bitcast(FP8X4),
+                        lhsT_scale=x_scales[:, TILES * s + t, tokens],
+                        rhs=w_words[:, g, cols].bitcast(FP8X4),
+                        rhs_scale=w_scales[:, g, cols],
+                        start=(g == 0),
+                        stop=(g == PASSES - 1),
+                    )
+            nc.vector.tensor_tensor(
+                out=v_grouped[s][:, cols, :],
+                in0=bank[:].rearrange("p t n -> p n t"),
+                in1=bias_rows[:, cols].unsqueeze(2).to_broadcast([P, P, PACK]),
+                op=ALU.add,
+            )
+
+        def quantise_v(s, h):
+            cols = slice(D_HEAD * h, D_HEAD * (h + 1))
+            nc.vector.quantize_mx(
+                out=v_codes[:, s, cols].bitcast(FP8X4),
+                scales=v_scales[:, s, cols],
+                in_=v_grouped[s][:, cols, :].rearrange("p n t -> p (n t)"),
+            )
+
+        def turn_qk(psum_turn, s, h):
+            turned = psum_turn.tile([P, 2, TOKENS], BF16, tag="turned")
+            for which, rows in enumerate((q_rows[s], k_rows[s])):
+                for i in range(TILES):
+                    nc.tensor.transpose(turned[:, which, P * i : P * (i + 1)], rows[:, TILES * h + i, :], ident_bf[:])
+            nc.scalar.copy(out=qk_cols[:, HEADS * s + h, :, :], in_=turned[:])
+
+        def sum_squares(rows, sums):
+            for u in range(UNITS):
+                nc.scalar.activation(out=squares[:, u, :], in_=rows[:, u, :], func=ACT.Square, accum_out=sums[:, u : u + 1])
+
+        def spread_q2(psum_turn, s):
+            pieces = q2_pieces[s]
+            rest = q2[s][:]
+            for n in range(PIECES):
+                piece = pieces[:, UNITS * n : UNITS * (n + 1)]
+                nc.vector.tensor_copy(out=piece, in_=rest)
+                if n < PIECES - 1:
+                    nc.vector.tensor_tensor(out=q2_rest[s][:, n, :], in0=rest, in1=piece, op=ALU.subtract)
+                    rest = q2_rest[s][:, n, :]
+            turned = psum_turn.tile([P, P], BF16, tag="turned")
+            nc.tensor.transpose(turned[:], pieces[:], ident_bf[:])
+            nc.scalar.copy(out=q2_piece_rows[s][:], in_=turned[:])
+
+        def half_distances(psum_score, s, h):
+            q_cols = qk_cols[:, HEADS * s + h, 0, :]
+            k_cols = qk_cols[:, HEADS * s + h, 1, :]
+            log_d2 = logs.tile([P, TILES, TOKENS], F32)
+            for t in range(TILES):
+                width = TOKENS - P * t
+                score = psum_score.tile([P, TOKENS], F32, tag="score")
+                nc.tensor.matmul(
+                    out=score[:, 0:width], lhsT=k_cols[:, P * t : P * (t + 1)], rhs=q_cols[:, P * t : TOKENS], start=True, stop=False
+                )
+                for i in range(t, TILES):
+                    u = TILES * h + i
+                    nc.tensor.matmul(
+                        out=score[:, P * (i - t) : P * (i - t + 1)],
+                        lhsT=selector[:, u : u + 1].to_broadcast([P, P]),
+                        rhs=q2_piece_rows[s][:],
+                        start=False,
+                        stop=(i == TILES - 1),
+                    )
+                nc.vector.tensor_scalar(
+                    out=log_d2[:, t, P * t : TOKENS],
+                    in0=score[:, 0:width],
+                    scalar1=minus_half_k2[s][:, TILES * h + t : TILES * h + t + 1],
+                    scalar2=-0.5 * D2_FLOOR,
+                    op0=ALU.add,
+                    op1=ALU.min,
+                )
+            return log_d2
+
+        def logarithms(log_d2):
+            for t in range(TILES):
+                live = log_d2[:, t, P * t : TOKENS]
+                nc.scalar.activation(out=live, in_=live, func=ACT.Ln, scale=-2.0)
+                diagonal = log_d2[:, t, P * t : P * (t + 1)]
+                nc.gpsimd.affine_select(
+                    out=diagonal, in_=diagonal, pattern=[[1, P]], compare_op=ALU.is_ge, fill=MASKED_LOG, base=0, channel_multiplier=-1
+                )
+
+        def weights(log_d2, grouped):
+            for i in range(TILES):
+                queries = slice(P * i, P * (i + 1))
+                nc.scalar.activation(
+                    out=grouped[:, queries, 0 : i + 1],
+                    in_=log_d2[:, 0 : i + 1, queries].rearrange("p t b -> p b t"),
+                    func=ACT.Sigmoid,
+                    scale=-0.5,
+                )
+
+        def quantise_w(grouped):
+            codes = ring.tile([P, TOKENS], U32, align_bytes=64)
+            scales = ring.tile([P, TOKENS], U8, align_bytes=64)
+            nc.vector.quantize_mx(out=codes[:].bitcast(FP8X4), scales=scales[:], in_=grouped[:].rearrange("p b t -> p (b t)"))
+            return codes, scales
+
+        def attend(psum_out, s, h, codes, scales):
+            cols = slice(D_HEAD * h, D_HEAD * (h + 1))
+            banks = []
+            for pair in range(TILES // 2):
+                bank = psum_out.tile([P, 2, D_HEAD], F32, tag="o_bank")
+                for half in range(2):
+                    queries = slice(P * (2 * pair + half), P * (2 * pair + half + 1))
+                    nc.tensor.matmul_mx(
+                        out=bank[:, half, :],
+                        lhsT=codes[:, queries].bitcast(FP8X4),
+                        lhsT_scale=scales[:, queries],
+                        rhs=v_codes[:, s, cols].bitcast(FP8X4),
+                        rhs_scale=v_scales[:, s, cols],
+                        start=True,
+                        stop=True,
+                    )
+                banks.append(bank)
+            return banks
+
+        def store(s, h, banks):
+            result = ring.tile([P, TILES, D_HEAD], F32)
+            for pair, bank in enumerate(banks):
+                nc.vector.tensor_copy(out=result[:, 2 * pair : 2 * pair + 2, :], in_=bank[:])
+            nc.sync.dma_start(
+                out=out[s].rearrange("(i p) n -> p i n", p=P)[:, :, D_HEAD * h : D_HEAD * (h + 1)], in_=result[:]
+            )
+
+        log_tiles = {}
+        with tc.psum_pool(name="turn", bufs=2) as psum_turn, tc.psum_pool(name="score", bufs=3) as psum_score:
+            for h in range(HEADS):
+                turn_qk(psum_turn, 0, h)
+            sum_squares(q_rows[0], q2[0])
+            sum_squares(k_rows[0], k2[0])
+            quantise_x_group(psum_turn, 0)
+            for h in range(HEADS):
+                project_chunk(0, 2 * h)
+                project_chunk(0, 2 * h + 1)
+                quantise_v(0, h)
+                turn_qk(psum_turn, 1, h)
+            sum_squares(q_rows[1], q2[1])
+            spread_q2(psum_turn, 0)
+            sum_squares(k_rows[1], k2[1])
+            quantise_x_group(psum_turn, 1)
+            spread_q2(psum_turn, 1)
+            for s in range(GROUPS):
+                nc.vector.tensor_scalar(out=minus_half_k2[s][:], in0=k2[s][:], scalar1=-0.5, scalar2=None, op0=ALU.mult)
+                for h in range(HEADS):
+                    log_tiles[(s, h)] = half_distances(psum_score, s, h)
+                for h in range(HEADS):
+                    logarithms(log_tiles[(s, h)])
+
+        with tc.psum_pool(name="out", bufs=4) as psum_out:
+            previous = None
+            for s in range(GROUPS):
+                for h in range(HEADS):
+                    grouped = w_grouped[(HEADS * s + h) % len(w_grouped)]
+                    weights(log_tiles[(s, h)], grouped)
+                    if s == 0:
+                        project_chunk(1, 2 * h)
+                    codes, scales = quantise_w(grouped)
+                    banks = attend(psum_out, s, h, codes, scales)
+                    if s == 0:
+                        project_chunk(1, 2 * h + 1)
+                        quantise_v(1, h)
+                    if previous is not None:
+                        store(*previous)
+                    previous = (s, h, banks)
+            store(*previous)

@@ -32,7 +32,7 @@ def tile_networklayer_pb_kernel(tc, q_pos, k_pos, x_grp, Wv_words, Wv_scales, bv
     nc = tc.nc
     with tc.tile_pool(name="keep", bufs=1) as keep, tc.tile_pool(name="ring", bufs=3) as ring, tc.tile_pool(
         name="logs", bufs=GROUPS * HEADS
-    ) as logs, tc.psum_pool(name="project", bufs=3) as psum_project:
+    ) as logs, tc.psum_pool(name="project", bufs=2) as psum_project, tc.manual_schedule():
         ident_bf = keep.tile([P, P], BF16)
         ident_f32 = keep.tile([P, P], F32)
         selector = keep.tile([P, UNITS], BF16)
@@ -147,11 +147,14 @@ def tile_networklayer_pb_kernel(tc, q_pos, k_pos, x_grp, Wv_words, Wv_scales, bv
                 in_=v_grouped[s][:, cols, :].rearrange("p n t -> p (n t)"),
             )
 
-        def turn_qk(psum_turn, s, h):
-            turned = psum_turn.tile([P, 2, TOKENS], BF16, tag="turned")
+        def turn_qk(psum_wide, s, h):
+            turned = psum_wide.tile([P, 2, TOKENS], BF16, tag="wide")
             for which, rows in enumerate((q_rows[s], k_rows[s])):
                 for i in range(TILES):
                     nc.tensor.transpose(turned[:, which, P * i : P * (i + 1)], rows[:, TILES * h + i, :], ident_bf[:])
+            return turned
+
+        def keep_qk(s, h, turned):
             nc.scalar.copy(out=qk_cols[:, HEADS * s + h, :, :], in_=turned[:])
 
         def sum_squares(rows, sums):
@@ -169,15 +172,15 @@ def tile_networklayer_pb_kernel(tc, q_pos, k_pos, x_grp, Wv_words, Wv_scales, bv
                     rest = q2_rest[s][:, n, :]
             turned = psum_turn.tile([P, P], BF16, tag="turned")
             nc.tensor.transpose(turned[:], pieces[:], ident_bf[:])
-            nc.scalar.copy(out=q2_piece_rows[s][:], in_=turned[:])
+            nc.vector.tensor_copy(out=q2_piece_rows[s][:], in_=turned[:])
 
-        def half_distances(psum_score, s, h):
+        def half_distances(psum_wide, s, h):
             q_cols = qk_cols[:, HEADS * s + h, 0, :]
             k_cols = qk_cols[:, HEADS * s + h, 1, :]
             log_d2 = logs.tile([P, TILES, TOKENS], F32)
             for t in range(TILES):
                 width = TOKENS - P * t
-                score = psum_score.tile([P, TOKENS], F32, tag="score")
+                score = psum_wide.tile([P, TOKENS], F32, tag="wide")
                 nc.tensor.matmul(
                     out=score[:, 0:width], lhsT=k_cols[:, P * t : P * (t + 1)], rhs=q_cols[:, P * t : TOKENS], start=True, stop=False
                 )
@@ -253,28 +256,30 @@ def tile_networklayer_pb_kernel(tc, q_pos, k_pos, x_grp, Wv_words, Wv_scales, bv
             )
 
         log_tiles = {}
-        with tc.psum_pool(name="turn", bufs=2) as psum_turn, tc.psum_pool(name="score", bufs=3) as psum_score:
-            for h in range(HEADS):
-                turn_qk(psum_turn, 0, h)
-            sum_squares(q_rows[0], q2[0])
-            sum_squares(k_rows[0], k2[0])
-            quantise_x_group(psum_turn, 0)
-            for h in range(HEADS):
-                project_chunk(0, 2 * h)
-                project_chunk(0, 2 * h + 1)
-                quantise_v(0, h)
-                turn_qk(psum_turn, 1, h)
-            sum_squares(q_rows[1], q2[1])
-            spread_q2(psum_turn, 0)
-            sum_squares(k_rows[1], k2[1])
-            quantise_x_group(psum_turn, 1)
-            spread_q2(psum_turn, 1)
+        with tc.psum_pool(name="wide", bufs=4) as psum_wide, tc.psum_pool(name="turn", bufs=2) as psum_turn:
+            for s in range(GROUPS):
+                turned = [turn_qk(psum_wide, s, h) for h in range(HEADS)]
+                sum_squares(q_rows[s], q2[s])
+                sum_squares(k_rows[s], k2[s])
+                for h in range(HEADS):
+                    keep_qk(s, h, turned[h])
+                quantise_x_group(psum_turn, s)
+                spread_q2(psum_turn, s)
+                if s == 0:
+                    for h in range(HEADS):
+                        project_chunk(s, 2 * h)
+                        project_chunk(s, 2 * h + 1)
+                        quantise_v(s, h)
             for s in range(GROUPS):
                 nc.vector.tensor_scalar(out=minus_half_k2[s][:], in0=k2[s][:], scalar1=-0.5, scalar2=None, op0=ALU.mult)
+            for s in range(GROUPS):
                 for h in range(HEADS):
-                    log_tiles[(s, h)] = half_distances(psum_score, s, h)
-                for h in range(HEADS):
+                    log_tiles[(s, h)] = half_distances(psum_wide, s, h)
                     logarithms(log_tiles[(s, h)])
+            for h in range(HEADS):
+                project_chunk(1, 2 * h)
+                project_chunk(1, 2 * h + 1)
+                quantise_v(1, h)
 
         with tc.psum_pool(name="out", bufs=4) as psum_out:
             previous = None
@@ -282,13 +287,8 @@ def tile_networklayer_pb_kernel(tc, q_pos, k_pos, x_grp, Wv_words, Wv_scales, bv
                 for h in range(HEADS):
                     grouped = w_grouped[(HEADS * s + h) % len(w_grouped)]
                     weights(log_tiles[(s, h)], grouped)
-                    if s == 0:
-                        project_chunk(1, 2 * h)
                     codes, scales = quantise_w(grouped)
                     banks = attend(psum_out, s, h, codes, scales)
-                    if s == 0:
-                        project_chunk(1, 2 * h + 1)
-                        quantise_v(1, h)
                     if previous is not None:
                         store(*previous)
                     previous = (s, h, banks)

@@ -30,9 +30,9 @@ MASKED_LOG = 1e30
 
 def tile_networklayer_pb_kernel(tc, q_pos, k_pos, x_grp, Wv_words, Wv_scales, bv, out):
     nc = tc.nc
-    with tc.tile_pool(name="keep", bufs=1) as keep, tc.tile_pool(name="ring", bufs=3) as ring, tc.tile_pool(
-        name="logs", bufs=GROUPS * HEADS
-    ) as logs, tc.psum_pool(name="project", bufs=2) as psum_project, tc.manual_schedule():
+    with tc.tile_pool(name="keep", bufs=1) as keep, tc.tile_pool(name="ring", bufs=3) as ring, tc.psum_pool(
+        name="project", bufs=2
+    ) as psum_project, tc.manual_schedule():
         ident_bf = keep.tile([P, P], BF16)
         ident_f32 = keep.tile([P, P], F32)
         selector = keep.tile([P, UNITS], BF16)
@@ -55,15 +55,15 @@ def tile_networklayer_pb_kernel(tc, q_pos, k_pos, x_grp, Wv_words, Wv_scales, bv
         q2_rest = [keep.tile([P, 2, UNITS], F32, name="q2_rest%d" % s) for s in range(GROUPS)]
         q2_pieces = [keep.tile([P, P], BF16, name="q2_pieces%d" % s) for s in range(GROUPS)]
         q2_piece_rows = [keep.tile([P, P], BF16, name="q2_piece_rows%d" % s) for s in range(GROUPS)]
-        w_grouped = [keep.tile([P, TOKENS, PACK], BF16, name="w_grouped%d" % n, align_bytes=64) for n in range(3)]
+        log_d2 = [keep.tile([P, TILES, HEADS, TOKENS], F32, name="log_d2_%d" % s) for s in range(GROUPS)]
+        w_grouped = keep.tile([P, TILES, HEADS, P, PACK], BF16, align_bytes=64)
 
         nc.vector.memset(w_scales[:].rearrange("p g n -> p (g n)").bitcast(I32), 0)
-        make_identity(nc, ident_bf[:])
         make_identity(nc, ident_f32[:])
+        make_identity(nc, ident_bf[:])
         for s in range(GROUPS):
             nc.vector.memset(q2_pieces[s][:].bitcast(I32), 0)
-        for tile in w_grouped:
-            nc.vector.memset(tile[:].rearrange("p b t -> p (b t)").bitcast(I32), 0)
+        nc.vector.memset(w_grouped[:].rearrange("p i h b t -> p (i h b t)").bitcast(I32), 0)
         nc.vector.tensor_tensor(out=selector[:], in0=ident_bf[:, 0:UNITS], in1=ident_bf[:, UNITS : 2 * UNITS], op=ALU.add)
         nc.vector.tensor_tensor(out=selector[:], in0=selector[:], in1=ident_bf[:, 2 * UNITS : 3 * UNITS], op=ALU.add)
         nc.vector.tensor_scalar(out=selector[:], in0=selector[:], scalar1=-0.5, scalar2=None, op0=ALU.mult)
@@ -71,15 +71,14 @@ def tile_networklayer_pb_kernel(tc, q_pos, k_pos, x_grp, Wv_words, Wv_scales, bv
         def load_rows(rows, source):
             nc.sync.dma_start(out=rows[:], in_=source.rearrange("h (i p) d -> p (h i) d", p=P))
 
-        def load_x(s):
-            for half in range(2):
-                tiles = slice(2 * half, 2 * half + 2)
-                nc.sync.dma_start(out=x_rows[s][:, tiles, :], in_=x_grp[s].rearrange("(t p) k -> p t k", p=P)[:, tiles, :])
+        def load_x(s, half):
+            tiles = slice(2 * half, 2 * half + 2)
+            nc.sync.dma_start(out=x_rows[s][:, tiles, :], in_=x_grp[s].rearrange("(t p) k -> p t k", p=P)[:, tiles, :])
 
-        nc.scalar.dma_start(out=bias_rows[:], in_=bv.partition_broadcast(P))
+        load_x(0, 0)
         load_rows(q_rows[0], q_pos[0])
+        load_x(0, 1)
         load_rows(k_rows[0], k_pos[0])
-        load_x(0)
         for quadrant in range(4):
             nc.sync.dma_start(
                 out=w_scales[32 * quadrant : 32 * quadrant + 4, :, :].bitcast(I32),
@@ -87,35 +86,27 @@ def tile_networklayer_pb_kernel(tc, q_pos, k_pos, x_grp, Wv_words, Wv_scales, bv
             )
         for g in range(PASSES):
             nc.sync.dma_start(out=w_words[:, g, :].bitcast(I32), in_=Wv_words[g].rearrange("p n t -> p (n t)").bitcast(I32))
+        nc.sync.dma_start(out=bias_rows[:], in_=bv.partition_broadcast(P))
         load_rows(q_rows[1], q_pos[1])
         load_rows(k_rows[1], k_pos[1])
-        load_x(1)
+        load_x(1, 0)
+        load_x(1, 1)
 
-        def regroup_x(psum_turn, s, t):
-            words = x_rows[s][:, t, :].bitcast(F32)
-            turned = psum_turn.tile([P, PASSES, 2, P], F32, tag="turned")
-            for g in range(PASSES):
-                for u in range(2):
-                    nc.tensor.transpose(turned[:, g, u, :], words[:, 256 * g + u : 256 * (g + 1) : 2], ident_f32[:])
-            x_grouped = ring.tile([P, PASSES, P, PACK], BF16, align_bytes=64)
-            nc.vector.tensor_copy(out=x_grouped[:].bitcast(F32), in_=turned[:].rearrange("p g u m -> p g m u"))
-            return x_grouped
-
-        def quantise_x(s, t, x_grouped):
+        def quantise_x_pair(psum_turn, s, pair):
+            x_grouped = ring.tile([P, 2, PASSES, P, PACK], BF16, align_bytes=64)
+            for n in range(2):
+                words = x_rows[s][:, 2 * pair + n, :].bitcast(F32)
+                turned = psum_turn.tile([P, PASSES, 2, P], F32, tag="turned")
+                for g in range(PASSES):
+                    for u in range(2):
+                        nc.tensor.transpose(turned[:, g, u, :], words[:, 256 * g + u : 256 * (g + 1) : 2], ident_f32[:])
+                nc.vector.tensor_copy(out=x_grouped[:, n].bitcast(F32), in_=turned[:].rearrange("p g u m -> p g m u"))
+            tiles = slice(TILES * s + 2 * pair, TILES * s + 2 * pair + 2)
             nc.vector.quantize_mx(
-                out=x_codes[:, TILES * s + t, :].bitcast(FP8X4),
-                scales=x_scales[:, TILES * s + t, :],
-                in_=x_grouped[:].rearrange("p g m j -> p (g m j)"),
+                out=x_codes[:, tiles, :].rearrange("p n w -> p (n w)").bitcast(FP8X4),
+                scales=x_scales[:, tiles, :].rearrange("p n w -> p (n w)"),
+                in_=x_grouped[:].rearrange("p n g m j -> p (n g m j)"),
             )
-
-        def quantise_x_group(psum_turn, s):
-            waiting = None
-            for t in range(TILES):
-                x_grouped = regroup_x(psum_turn, s, t)
-                if waiting is not None:
-                    quantise_x(s, t - 1, waiting)
-                waiting = x_grouped
-            quantise_x(s, TILES - 1, waiting)
 
         def project_chunk(s, j):
             cols = slice(P * j, P * (j + 1))
@@ -139,13 +130,16 @@ def tile_networklayer_pb_kernel(tc, q_pos, k_pos, x_grp, Wv_words, Wv_scales, bv
                 op=ALU.add,
             )
 
-        def quantise_v(s, h):
-            cols = slice(D_HEAD * h, D_HEAD * (h + 1))
-            nc.vector.quantize_mx(
-                out=v_codes[:, s, cols].bitcast(FP8X4),
-                scales=v_scales[:, s, cols],
-                in_=v_grouped[s][:, cols, :].rearrange("p n t -> p (n t)"),
-            )
+        def project(s):
+            for half in range(2):
+                for j in range(4 * half, 4 * half + 4):
+                    project_chunk(s, j)
+                cols = slice(2 * D_HEAD * half, 2 * D_HEAD * (half + 1))
+                nc.vector.quantize_mx(
+                    out=v_codes[:, s, cols].bitcast(FP8X4),
+                    scales=v_scales[:, s, cols],
+                    in_=v_grouped[s][:, cols, :].rearrange("p n t -> p (n t)"),
+                )
 
         def turn_qk(psum_wide, s, h):
             turned = psum_wide.tile([P, 2, TOKENS], BF16, tag="wide")
@@ -153,9 +147,6 @@ def tile_networklayer_pb_kernel(tc, q_pos, k_pos, x_grp, Wv_words, Wv_scales, bv
                 for i in range(TILES):
                     nc.tensor.transpose(turned[:, which, P * i : P * (i + 1)], rows[:, TILES * h + i, :], ident_bf[:])
             return turned
-
-        def keep_qk(s, h, turned):
-            nc.scalar.copy(out=qk_cols[:, HEADS * s + h, :, :], in_=turned[:])
 
         def sum_squares(rows, sums):
             for u in range(UNITS):
@@ -166,20 +157,28 @@ def tile_networklayer_pb_kernel(tc, q_pos, k_pos, x_grp, Wv_words, Wv_scales, bv
             rest = q2[s][:]
             for n in range(PIECES):
                 piece = pieces[:, UNITS * n : UNITS * (n + 1)]
-                nc.vector.tensor_copy(out=piece, in_=rest)
+                nc.gpsimd.tensor_copy(out=piece, in_=rest)
                 if n < PIECES - 1:
-                    nc.vector.tensor_tensor(out=q2_rest[s][:, n, :], in0=rest, in1=piece, op=ALU.subtract)
+                    nc.gpsimd.tensor_tensor(out=q2_rest[s][:, n, :], in0=rest, in1=piece, op=ALU.subtract)
                     rest = q2_rest[s][:, n, :]
             turned = psum_turn.tile([P, P], BF16, tag="turned")
             nc.tensor.transpose(turned[:], pieces[:], ident_bf[:])
             nc.vector.tensor_copy(out=q2_piece_rows[s][:], in_=turned[:])
 
-        def half_distances(psum_wide, s, h):
-            q_cols = qk_cols[:, HEADS * s + h, 0, :]
-            k_cols = qk_cols[:, HEADS * s + h, 1, :]
-            log_d2 = logs.tile([P, TILES, TOKENS], F32)
-            for t in range(TILES):
-                width = TOKENS - P * t
+        def prepare_qk(psum_wide, psum_turn, s):
+            turned = [turn_qk(psum_wide, s, h) for h in range(HEADS)]
+            sum_squares(q_rows[s], q2[s])
+            spread_q2(psum_turn, s)
+            sum_squares(k_rows[s], k2[s])
+            nc.gpsimd.tensor_scalar(out=minus_half_k2[s][:], in0=k2[s][:], scalar1=-0.5, scalar2=0.0, op0=ALU.mult, op1=ALU.add)
+            for h in range(HEADS):
+                nc.scalar.copy(out=qk_cols[:, HEADS * s + h, :, :], in_=turned[h][:])
+
+        def logarithms(psum_wide, s, t):
+            width = TOKENS - P * t
+            for h in range(HEADS):
+                q_cols = qk_cols[:, HEADS * s + h, 0, :]
+                k_cols = qk_cols[:, HEADS * s + h, 1, :]
                 score = psum_wide.tile([P, TOKENS], F32, tag="wide")
                 nc.tensor.matmul(
                     out=score[:, 0:width], lhsT=k_cols[:, P * t : P * (t + 1)], rhs=q_cols[:, P * t : TOKENS], start=True, stop=False
@@ -194,102 +193,76 @@ def tile_networklayer_pb_kernel(tc, q_pos, k_pos, x_grp, Wv_words, Wv_scales, bv
                         stop=(i == TILES - 1),
                     )
                 nc.vector.tensor_scalar(
-                    out=log_d2[:, t, P * t : TOKENS],
+                    out=log_d2[s][:, t, h, P * t : TOKENS],
                     in0=score[:, 0:width],
                     scalar1=minus_half_k2[s][:, TILES * h + t : TILES * h + t + 1],
                     scalar2=-0.5 * D2_FLOOR,
                     op0=ALU.add,
                     op1=ALU.min,
                 )
-            return log_d2
-
-        def logarithms(log_d2):
-            for t in range(TILES):
-                live = log_d2[:, t, P * t : TOKENS]
-                nc.scalar.activation(out=live, in_=live, func=ACT.Ln, scale=-2.0)
-                diagonal = log_d2[:, t, P * t : P * (t + 1)]
+            live = log_d2[s][:, t, :, P * t : TOKENS]
+            nc.scalar.activation(out=live, in_=live, func=ACT.Ln, scale=-2.0)
+            for h in range(HEADS):
+                diagonal = log_d2[s][:, t, h, P * t : P * (t + 1)]
                 nc.gpsimd.affine_select(
                     out=diagonal, in_=diagonal, pattern=[[1, P]], compare_op=ALU.is_ge, fill=MASKED_LOG, base=0, channel_multiplier=-1
                 )
 
-        def weights(log_d2, grouped):
-            for i in range(TILES):
-                queries = slice(P * i, P * (i + 1))
-                nc.scalar.activation(
-                    out=grouped[:, queries, 0 : i + 1],
-                    in_=log_d2[:, 0 : i + 1, queries].rearrange("p t b -> p b t"),
-                    func=ACT.Sigmoid,
-                    scale=-0.5,
-                )
-
-        def quantise_w(grouped):
-            codes = ring.tile([P, TOKENS], U32, align_bytes=64)
-            scales = ring.tile([P, TOKENS], U8, align_bytes=64)
-            nc.vector.quantize_mx(out=codes[:].bitcast(FP8X4), scales=scales[:], in_=grouped[:].rearrange("p b t -> p (b t)"))
-            return codes, scales
-
-        def attend(psum_out, s, h, codes, scales):
-            cols = slice(D_HEAD * h, D_HEAD * (h + 1))
+        def attend(psum_out, s, i):
+            queries = slice(P * i, P * (i + 1))
+            nc.scalar.activation(
+                out=w_grouped[:, i, :, :, 0 : i + 1],
+                in_=log_d2[s][:, 0 : i + 1, :, queries].rearrange("p t h b -> p h b t"),
+                func=ACT.Sigmoid,
+                scale=-0.5,
+            )
+            codes = ring.tile([P, HEADS * P], U32, align_bytes=64)
+            scales = ring.tile([P, HEADS * P], U8, align_bytes=64)
+            nc.vector.quantize_mx(
+                out=codes[:].bitcast(FP8X4), scales=scales[:], in_=w_grouped[:, i].rearrange("p h b t -> p (h b t)")
+            )
             banks = []
-            for pair in range(TILES // 2):
+            for pair in range(HEADS // 2):
                 bank = psum_out.tile([P, 2, D_HEAD], F32, tag="o_bank")
                 for half in range(2):
-                    queries = slice(P * (2 * pair + half), P * (2 * pair + half + 1))
+                    h = 2 * pair + half
                     nc.tensor.matmul_mx(
                         out=bank[:, half, :],
-                        lhsT=codes[:, queries].bitcast(FP8X4),
-                        lhsT_scale=scales[:, queries],
-                        rhs=v_codes[:, s, cols].bitcast(FP8X4),
-                        rhs_scale=v_scales[:, s, cols],
+                        lhsT=codes[:, P * h : P * (h + 1)].bitcast(FP8X4),
+                        lhsT_scale=scales[:, P * h : P * (h + 1)],
+                        rhs=v_codes[:, s, D_HEAD * h : D_HEAD * (h + 1)].bitcast(FP8X4),
+                        rhs_scale=v_scales[:, s, D_HEAD * h : D_HEAD * (h + 1)],
                         start=True,
                         stop=True,
                     )
                 banks.append(bank)
             return banks
 
-        def store(s, h, banks):
-            result = ring.tile([P, TILES, D_HEAD], F32)
+        def store(s, i, banks):
+            result = ring.tile([P, HEADS // 2, 2 * D_HEAD], F32)
             for pair, bank in enumerate(banks):
-                nc.vector.tensor_copy(out=result[:, 2 * pair : 2 * pair + 2, :], in_=bank[:])
-            nc.sync.dma_start(
-                out=out[s].rearrange("(i p) n -> p i n", p=P)[:, :, D_HEAD * h : D_HEAD * (h + 1)], in_=result[:]
-            )
+                nc.vector.tensor_copy(out=result[:, pair, :], in_=bank[:].rearrange("p e n -> p (e n)"))
+            nc.sync.dma_start(out=out[s, P * i : P * (i + 1), :], in_=result[:].rearrange("p e n -> p (e n)"))
 
-        log_tiles = {}
         with tc.psum_pool(name="wide", bufs=4) as psum_wide, tc.psum_pool(name="turn", bufs=2) as psum_turn:
+            for pair in range(TILES // 2):
+                quantise_x_pair(psum_turn, 0, pair)
+            prepare_qk(psum_wide, psum_turn, 0)
+            project(0)
+            prepare_qk(psum_wide, psum_turn, 1)
+            for pair in range(TILES // 2):
+                quantise_x_pair(psum_turn, 1, pair)
             for s in range(GROUPS):
-                turned = [turn_qk(psum_wide, s, h) for h in range(HEADS)]
-                sum_squares(q_rows[s], q2[s])
-                sum_squares(k_rows[s], k2[s])
-                for h in range(HEADS):
-                    keep_qk(s, h, turned[h])
-                quantise_x_group(psum_turn, s)
-                spread_q2(psum_turn, s)
-                if s == 0:
-                    for h in range(HEADS):
-                        project_chunk(s, 2 * h)
-                        project_chunk(s, 2 * h + 1)
-                        quantise_v(s, h)
-            for s in range(GROUPS):
-                nc.vector.tensor_scalar(out=minus_half_k2[s][:], in0=k2[s][:], scalar1=-0.5, scalar2=None, op0=ALU.mult)
-            for s in range(GROUPS):
-                for h in range(HEADS):
-                    log_tiles[(s, h)] = half_distances(psum_wide, s, h)
-                    logarithms(log_tiles[(s, h)])
-            for h in range(HEADS):
-                project_chunk(1, 2 * h)
-                project_chunk(1, 2 * h + 1)
-                quantise_v(1, h)
+                for t in range(TILES):
+                    logarithms(psum_wide, s, t)
+            project(1)
 
         with tc.psum_pool(name="out", bufs=4) as psum_out:
             previous = None
             for s in range(GROUPS):
-                for h in range(HEADS):
-                    grouped = w_grouped[(HEADS * s + h) % len(w_grouped)]
-                    weights(log_tiles[(s, h)], grouped)
-                    codes, scales = quantise_w(grouped)
-                    banks = attend(psum_out, s, h, codes, scales)
+                for i in reversed(range(TILES)):
+                    banks = attend(psum_out, s, i)
                     if previous is not None:
                         store(*previous)
-                    previous = (s, h, banks)
+                    previous = (s, i, banks)
             store(*previous)

@@ -31,8 +31,8 @@ MASKED_LOG = 1e30
 def tile_networklayer_pb_kernel(tc, q_pos, k_pos, x_grp, Wv_words, Wv_scales, bv, out):
     nc = tc.nc
     with tc.tile_pool(name="keep", bufs=1) as keep, tc.tile_pool(name="ring", bufs=3) as ring, tc.psum_pool(
-        name="project", bufs=2
-    ) as psum_project, tc.manual_schedule():
+        name="work", bufs=4
+    ) as psum_work, tc.manual_schedule():
         ident_bf = keep.tile([P, P], BF16)
         ident_f32 = keep.tile([P, P], F32)
         selector = keep.tile([P, UNITS], BF16)
@@ -92,11 +92,11 @@ def tile_networklayer_pb_kernel(tc, q_pos, k_pos, x_grp, Wv_words, Wv_scales, bv
         load_x(1, 0)
         load_x(1, 1)
 
-        def quantise_x_pair(psum_turn, s, pair):
+        def quantise_x_pair(s, pair):
             x_grouped = ring.tile([P, 2, PASSES, P, PACK], BF16, align_bytes=64)
             for n in range(2):
                 words = x_rows[s][:, 2 * pair + n, :].bitcast(F32)
-                turned = psum_turn.tile([P, PASSES, 2, P], F32, tag="turned")
+                turned = psum_work.tile([P, PASSES, 2, P], F32, tag="work")
                 for g in range(PASSES):
                     for u in range(2):
                         nc.tensor.transpose(turned[:, g, u, :], words[:, 256 * g + u : 256 * (g + 1) : 2], ident_f32[:])
@@ -110,7 +110,7 @@ def tile_networklayer_pb_kernel(tc, q_pos, k_pos, x_grp, Wv_words, Wv_scales, bv
 
         def project_chunk(s, j):
             cols = slice(P * j, P * (j + 1))
-            bank = psum_project.tile([P, TILES, P], F32, tag="bank")
+            bank = psum_work.tile([P, TILES, P], F32, tag="work")
             for t in range(TILES):
                 for g in range(PASSES):
                     tokens = slice(P * g, P * (g + 1))
@@ -152,7 +152,7 @@ def tile_networklayer_pb_kernel(tc, q_pos, k_pos, x_grp, Wv_words, Wv_scales, bv
             for u in range(UNITS):
                 nc.scalar.activation(out=squares[:, u, :], in_=rows[:, u, :], func=ACT.Square, accum_out=sums[:, u : u + 1])
 
-        def spread_q2(psum_turn, s):
+        def split_q2(s):
             pieces = q2_pieces[s]
             rest = q2[s][:]
             for n in range(PIECES):
@@ -161,14 +161,16 @@ def tile_networklayer_pb_kernel(tc, q_pos, k_pos, x_grp, Wv_words, Wv_scales, bv
                 if n < PIECES - 1:
                     nc.gpsimd.tensor_tensor(out=q2_rest[s][:, n, :], in0=rest, in1=piece, op=ALU.subtract)
                     rest = q2_rest[s][:, n, :]
-            turned = psum_turn.tile([P, P], BF16, tag="turned")
-            nc.tensor.transpose(turned[:], pieces[:], ident_bf[:])
+
+        def turn_q2(s):
+            turned = psum_work.tile([P, P], BF16, tag="work")
+            nc.tensor.transpose(turned[:], q2_pieces[s][:], ident_bf[:])
             nc.vector.tensor_copy(out=q2_piece_rows[s][:], in_=turned[:])
 
-        def prepare_qk(psum_wide, psum_turn, s):
+        def prepare_qk(psum_wide, s):
             turned = [turn_qk(psum_wide, s, h) for h in range(HEADS)]
             sum_squares(q_rows[s], q2[s])
-            spread_q2(psum_turn, s)
+            split_q2(s)
             sum_squares(k_rows[s], k2[s])
             nc.gpsimd.tensor_scalar(out=minus_half_k2[s][:], in0=k2[s][:], scalar1=-0.5, scalar2=0.0, op0=ALU.mult, op1=ALU.add)
             for h in range(HEADS):
@@ -244,14 +246,16 @@ def tile_networklayer_pb_kernel(tc, q_pos, k_pos, x_grp, Wv_words, Wv_scales, bv
                 nc.vector.tensor_copy(out=result[:, pair, :], in_=bank[:].rearrange("p e n -> p (e n)"))
             nc.sync.dma_start(out=out[s, P * i : P * (i + 1), :], in_=result[:].rearrange("p e n -> p (e n)"))
 
-        with tc.psum_pool(name="wide", bufs=4) as psum_wide, tc.psum_pool(name="turn", bufs=2) as psum_turn:
+        with tc.psum_pool(name="wide", bufs=4) as psum_wide:
             for pair in range(TILES // 2):
-                quantise_x_pair(psum_turn, 0, pair)
-            prepare_qk(psum_wide, psum_turn, 0)
+                quantise_x_pair(0, pair)
+            prepare_qk(psum_wide, 0)
             project(0)
-            prepare_qk(psum_wide, psum_turn, 1)
+            turn_q2(0)
+            prepare_qk(psum_wide, 1)
             for pair in range(TILES // 2):
-                quantise_x_pair(psum_turn, 1, pair)
+                quantise_x_pair(1, pair)
+            turn_q2(1)
             for s in range(GROUPS):
                 for t in range(TILES):
                     logarithms(psum_wide, s, t)

@@ -1,3 +1,5 @@
+import math
+
 import concourse.mybir as mybir
 from concourse.masks import make_identity
 
@@ -25,6 +27,7 @@ CHUNKS = D_MODEL // P
 UNITS = HEADS * TILES
 PIECES = 3
 D2_FLOOR = 1e-12
+LOG_FLOOR = math.log(D2_FLOOR)
 MASKED_LOG = 1e30
 
 
@@ -36,6 +39,10 @@ def tile_networklayer_pb_kernel(tc, q_pos, k_pos, x_grp, Wv_words, Wv_scales, bv
         ident_bf = keep.tile([P, P], BF16)
         ident_f32 = keep.tile([P, P], F32)
         selector = keep.tile([P, UNITS], BF16)
+        one = keep.tile([P, 1], F32)
+        log_one = keep.tile([P, 1], F32)
+        ones = keep.tile([P, P], BF16)
+        bias_first = keep.tile([P, D_MODEL], BF16)
         bias_rows = keep.tile([P, D_MODEL], BF16)
         q_rows = [keep.tile([P, UNITS, P], BF16, name="q_rows%d" % s) for s in range(GROUPS)]
         k_rows = [keep.tile([P, UNITS, P], BF16, name="k_rows%d" % s) for s in range(GROUPS)]
@@ -51,16 +58,20 @@ def tile_networklayer_pb_kernel(tc, q_pos, k_pos, x_grp, Wv_words, Wv_scales, bv
         squares = keep.tile([P, UNITS, P], BF16)
         q2 = [keep.tile([P, UNITS], F32, name="q2_%d" % s) for s in range(GROUPS)]
         k2 = [keep.tile([P, UNITS], F32, name="k2_%d" % s) for s in range(GROUPS)]
-        minus_half_k2 = [keep.tile([P, UNITS], F32, name="minus_half_k2_%d" % s) for s in range(GROUPS)]
         q2_rest = [keep.tile([P, 2, UNITS], F32, name="q2_rest%d" % s) for s in range(GROUPS)]
         q2_pieces = [keep.tile([P, P], BF16, name="q2_pieces%d" % s) for s in range(GROUPS)]
         q2_piece_rows = [keep.tile([P, P], BF16, name="q2_piece_rows%d" % s) for s in range(GROUPS)]
-        log_d2 = [keep.tile([P, TILES, HEADS, TOKENS], F32, name="log_d2_%d" % s) for s in range(GROUPS)]
+        log_d2 = [keep.tile([P, TILES, TILES, HEADS, P], F32, name="log_d2_%d" % s) for s in range(GROUPS)]
+        k_squares = keep.tile([P, UNITS, P], F32)
         w_grouped = keep.tile([P, TILES, HEADS, P, PACK], BF16, align_bytes=64)
 
+        nc.vector.memset(one[:], 1.0)
+        nc.scalar.activation(out=log_one[:], in_=one[:], func=ACT.Ln)
         nc.vector.memset(w_scales[:].rearrange("p g n -> p (g n)").bitcast(I32), 0)
         make_identity(nc, ident_f32[:])
         make_identity(nc, ident_bf[:])
+        nc.vector.memset(ones[:], 1.0)
+        nc.vector.memset(bias_first[:].bitcast(I32), 0)
         for s in range(GROUPS):
             nc.vector.memset(q2_pieces[s][:].bitcast(I32), 0)
         nc.vector.memset(w_grouped[:].rearrange("p i h b t -> p (i h b t)").bitcast(I32), 0)
@@ -75,10 +86,15 @@ def tile_networklayer_pb_kernel(tc, q_pos, k_pos, x_grp, Wv_words, Wv_scales, bv
             tiles = slice(2 * half, 2 * half + 2)
             nc.sync.dma_start(out=x_rows[s][:, tiles, :], in_=x_grp[s].rearrange("(t p) k -> p t k", p=P)[:, tiles, :])
 
-        load_x(0, 0)
         load_rows(q_rows[0], q_pos[0])
-        load_x(0, 1)
         load_rows(k_rows[0], k_pos[0])
+        load_x(0, 0)
+        load_x(0, 1)
+        load_rows(q_rows[1], q_pos[1])
+        load_rows(k_rows[1], k_pos[1])
+        load_x(1, 0)
+        load_x(1, 1)
+        nc.sync.dma_start(out=bias_first[0:1, :], in_=bv.unsqueeze(0))
         for quadrant in range(4):
             nc.sync.dma_start(
                 out=w_scales[32 * quadrant : 32 * quadrant + 4, :, :].bitcast(I32),
@@ -86,21 +102,27 @@ def tile_networklayer_pb_kernel(tc, q_pos, k_pos, x_grp, Wv_words, Wv_scales, bv
             )
         for g in range(PASSES):
             nc.sync.dma_start(out=w_words[:, g, :].bitcast(I32), in_=Wv_words[g].rearrange("p n t -> p (n t)").bitcast(I32))
-        nc.sync.dma_start(out=bias_rows[:], in_=bv.partition_broadcast(P))
-        load_rows(q_rows[1], q_pos[1])
-        load_rows(k_rows[1], k_pos[1])
-        load_x(1, 0)
-        load_x(1, 1)
 
-        def quantise_x_pair(s, pair):
+        def spread_bias(copy):
+            for half in range(2):
+                cols = slice(4 * P * half, 4 * P * (half + 1))
+                bank = psum_work.tile([P, 4 * P], F32, tag="work")
+                nc.tensor.matmul(out=bank[:], lhsT=ones[:], rhs=bias_first[:, cols], start=True, stop=True)
+                copy(out=bias_rows[:, cols], in_=bank[:])
+
+        def turn_x(s, n, x_grouped, copy):
+            words = x_rows[s][:, n, :].bitcast(F32)
+            turned = psum_work.tile([P, PASSES, 2, P], F32, tag="work")
+            for g in range(PASSES):
+                for u in range(2):
+                    nc.tensor.transpose(turned[:, g, u, :], words[:, 256 * g + u : 256 * (g + 1) : 2], ident_f32[:])
+            copy(out=x_grouped[:, n % 2].bitcast(F32), in_=turned[:].rearrange("p g u m -> p g m u"))
+
+        def new_x_pair():
             x_grouped = ring.tile([P, 2, PASSES, P, PACK], BF16, align_bytes=64)
-            for n in range(2):
-                words = x_rows[s][:, 2 * pair + n, :].bitcast(F32)
-                turned = psum_work.tile([P, PASSES, 2, P], F32, tag="work")
-                for g in range(PASSES):
-                    for u in range(2):
-                        nc.tensor.transpose(turned[:, g, u, :], words[:, 256 * g + u : 256 * (g + 1) : 2], ident_f32[:])
-                nc.vector.tensor_copy(out=x_grouped[:, n].bitcast(F32), in_=turned[:].rearrange("p g u m -> p g m u"))
+            return x_grouped
+
+        def quantise_x_pair(s, pair, x_grouped):
             tiles = slice(TILES * s + 2 * pair, TILES * s + 2 * pair + 2)
             nc.vector.quantize_mx(
                 out=x_codes[:, tiles, :].rearrange("p n w -> p (n w)").bitcast(FP8X4),
@@ -123,6 +145,10 @@ def tile_networklayer_pb_kernel(tc, q_pos, k_pos, x_grp, Wv_words, Wv_scales, bv
                         start=(g == 0),
                         stop=(g == PASSES - 1),
                     )
+            return bank
+
+        def add_bias(s, j, bank):
+            cols = slice(P * j, P * (j + 1))
             nc.vector.tensor_tensor(
                 out=v_grouped[s][:, cols, :],
                 in0=bank[:].rearrange("p t n -> p n t"),
@@ -130,27 +156,42 @@ def tile_networklayer_pb_kernel(tc, q_pos, k_pos, x_grp, Wv_words, Wv_scales, bv
                 op=ALU.add,
             )
 
-        def project(s):
-            for half in range(2):
-                for j in range(4 * half, 4 * half + 4):
-                    project_chunk(s, j)
-                cols = slice(2 * D_HEAD * half, 2 * D_HEAD * (half + 1))
-                nc.vector.quantize_mx(
-                    out=v_codes[:, s, cols].bitcast(FP8X4),
-                    scales=v_scales[:, s, cols],
-                    in_=v_grouped[s][:, cols, :].rearrange("p n t -> p (n t)"),
-                )
+        def quantise_v(s, half):
+            cols = slice(2 * D_HEAD * half, 2 * D_HEAD * (half + 1))
+            nc.vector.quantize_mx(
+                out=v_codes[:, s, cols].bitcast(FP8X4),
+                scales=v_scales[:, s, cols],
+                in_=v_grouped[s][:, cols, :].rearrange("p n t -> p (n t)"),
+            )
 
-        def turn_qk(psum_wide, s, h):
-            turned = psum_wide.tile([P, 2, TOKENS], BF16, tag="wide")
+        def turn_qk(pool, tag, s, h):
+            turned = pool.tile([P, 2, TOKENS], BF16, tag=tag)
             for which, rows in enumerate((q_rows[s], k_rows[s])):
                 for i in range(TILES):
                     nc.tensor.transpose(turned[:, which, P * i : P * (i + 1)], rows[:, TILES * h + i, :], ident_bf[:])
             return turned
 
-        def sum_squares(rows, sums):
-            for u in range(UNITS):
+        def sum_squares(rows, sums, units):
+            for u in units:
                 nc.scalar.activation(out=squares[:, u, :], in_=rows[:, u, :], func=ACT.Square, accum_out=sums[:, u : u + 1])
+
+        def square_k(s, half):
+            for quarter in range(2):
+                some = slice(UNITS // 4 * (2 * half + quarter), UNITS // 4 * (2 * half + quarter + 1))
+                nc.gpsimd.tensor_tensor(
+                    out=k_squares[:, some, :], in0=k_rows[s][:, some, :], in1=k_rows[s][:, some, :], op=ALU.mult
+                )
+
+        def add_k_squares(s, half):
+            units = slice(UNITS // 2 * half, UNITS // 2 * (half + 1))
+            part = k_squares[:, units, :]
+            width = P // 2
+            while width > 1:
+                nc.gpsimd.tensor_tensor(
+                    out=part[:, :, 0:width], in0=part[:, :, 0:width], in1=part[:, :, width : 2 * width], op=ALU.add
+                )
+                width //= 2
+            nc.gpsimd.tensor_tensor(out=k2[s][:, units].unsqueeze(2), in0=part[:, :, 0:1], in1=part[:, :, 1:2], op=ALU.add)
 
         def split_q2(s):
             pieces = q2_pieces[s]
@@ -167,62 +208,64 @@ def tile_networklayer_pb_kernel(tc, q_pos, k_pos, x_grp, Wv_words, Wv_scales, bv
             nc.tensor.transpose(turned[:], q2_pieces[s][:], ident_bf[:])
             nc.vector.tensor_copy(out=q2_piece_rows[s][:], in_=turned[:])
 
-        def prepare_qk(psum_wide, s):
-            turned = [turn_qk(psum_wide, s, h) for h in range(HEADS)]
-            sum_squares(q_rows[s], q2[s])
-            split_q2(s)
-            sum_squares(k_rows[s], k2[s])
-            nc.gpsimd.tensor_scalar(out=minus_half_k2[s][:], in0=k2[s][:], scalar1=-0.5, scalar2=0.0, op0=ALU.mult, op1=ALU.add)
-            for h in range(HEADS):
-                nc.scalar.copy(out=qk_cols[:, HEADS * s + h, :, :], in_=turned[h][:])
-
-        def logarithms(psum_wide, s, t):
+        def logarithm(psum_wide, s, h, t):
             width = TOKENS - P * t
-            for h in range(HEADS):
-                q_cols = qk_cols[:, HEADS * s + h, 0, :]
-                k_cols = qk_cols[:, HEADS * s + h, 1, :]
-                score = psum_wide.tile([P, TOKENS], F32, tag="wide")
+            q_cols = qk_cols[:, HEADS * s + h, 0, :]
+            k_cols = qk_cols[:, HEADS * s + h, 1, :]
+            score = psum_wide.tile([P, TOKENS], F32, tag="wide")
+            nc.tensor.matmul(
+                out=score[:, 0:width], lhsT=k_cols[:, P * t : P * (t + 1)], rhs=q_cols[:, P * t : TOKENS], start=True, stop=False
+            )
+            for i in range(t, TILES):
+                u = TILES * h + i
                 nc.tensor.matmul(
-                    out=score[:, 0:width], lhsT=k_cols[:, P * t : P * (t + 1)], rhs=q_cols[:, P * t : TOKENS], start=True, stop=False
+                    out=score[:, P * (i - t) : P * (i - t + 1)],
+                    lhsT=selector[:, u : u + 1].to_broadcast([P, P]),
+                    rhs=q2_piece_rows[s][:],
+                    start=False,
+                    stop=(i == TILES - 1),
                 )
-                for i in range(t, TILES):
-                    u = TILES * h + i
-                    nc.tensor.matmul(
-                        out=score[:, P * (i - t) : P * (i - t + 1)],
-                        lhsT=selector[:, u : u + 1].to_broadcast([P, P]),
-                        rhs=q2_piece_rows[s][:],
-                        start=False,
-                        stop=(i == TILES - 1),
-                    )
-                nc.vector.tensor_scalar(
-                    out=log_d2[s][:, t, h, P * t : TOKENS],
-                    in0=score[:, 0:width],
-                    scalar1=minus_half_k2[s][:, TILES * h + t : TILES * h + t + 1],
-                    scalar2=-0.5 * D2_FLOOR,
-                    op0=ALU.add,
-                    op1=ALU.min,
-                )
-            live = log_d2[s][:, t, :, P * t : TOKENS]
-            nc.scalar.activation(out=live, in_=live, func=ACT.Ln, scale=-2.0)
-            for h in range(HEADS):
-                diagonal = log_d2[s][:, t, h, P * t : P * (t + 1)]
-                nc.gpsimd.affine_select(
-                    out=diagonal, in_=diagonal, pattern=[[1, P]], compare_op=ALU.is_ge, fill=MASKED_LOG, base=0, channel_multiplier=-1
-                )
+            nc.scalar.activation(
+                out=log_d2[s][:, t:TILES, t, h, :],
+                in_=score[:, 0:width].rearrange("p (i b) -> p i b", b=P),
+                func=ACT.Ln,
+                bias=k2[s][:, TILES * h + t : TILES * h + t + 1],
+                scale=-2.0,
+            )
 
-        def attend(psum_out, s, i):
-            queries = slice(P * i, P * (i + 1))
+        def floor(s, i):
+            live = log_d2[s][:, i, 0 : i + 1, :, :].rearrange("p t h b -> p (t h b)")
+            nc.vector.tensor_scalar(out=live, in0=live, scalar1=LOG_FLOOR, scalar2=None, op0=ALU.max)
+
+        def mask(s, i):
+            diagonal = log_d2[s][:, i, i, :, :]
+            nc.gpsimd.affine_select(
+                out=diagonal,
+                in_=diagonal,
+                pattern=[[0, HEADS], [1, P]],
+                compare_op=ALU.is_ge,
+                fill=MASKED_LOG,
+                base=0,
+                channel_multiplier=-1,
+            )
+
+        def weigh(s, i):
             nc.scalar.activation(
                 out=w_grouped[:, i, :, :, 0 : i + 1],
-                in_=log_d2[s][:, 0 : i + 1, :, queries].rearrange("p t h b -> p h b t"),
+                in_=log_d2[s][:, i, 0 : i + 1, :, :].rearrange("p t h b -> p h b t"),
                 func=ACT.Sigmoid,
                 scale=-0.5,
             )
+
+        def quantise_w(i):
             codes = ring.tile([P, HEADS * P], U32, align_bytes=64)
             scales = ring.tile([P, HEADS * P], U8, align_bytes=64)
             nc.vector.quantize_mx(
                 out=codes[:].bitcast(FP8X4), scales=scales[:], in_=w_grouped[:, i].rearrange("p h b t -> p (h b t)")
             )
+            return codes, scales
+
+        def attend(psum_out, s, codes, scales):
             banks = []
             for pair in range(HEADS // 2):
                 bank = psum_out.tile([P, 2, D_HEAD], F32, tag="o_bank")
@@ -240,33 +283,87 @@ def tile_networklayer_pb_kernel(tc, q_pos, k_pos, x_grp, Wv_words, Wv_scales, bv
                 banks.append(bank)
             return banks
 
-        def store(s, i, banks):
+        def store(s, i, banks, copies):
             result = ring.tile([P, HEADS // 2, 2 * D_HEAD], F32)
             for pair, bank in enumerate(banks):
-                nc.vector.tensor_copy(out=result[:, pair, :], in_=bank[:].rearrange("p e n -> p (e n)"))
+                copies[pair](out=result[:, pair, :], in_=bank[:].rearrange("p e n -> p (e n)"))
             nc.sync.dma_start(out=out[s, P * i : P * (i + 1), :], in_=result[:].rearrange("p e n -> p (e n)"))
 
+        vcopy, scopy = nc.vector.tensor_copy, nc.scalar.copy
         with tc.psum_pool(name="wide", bufs=4) as psum_wide:
-            for pair in range(TILES // 2):
-                quantise_x_pair(0, pair)
-            prepare_qk(psum_wide, 0)
-            project(0)
+            turned = [turn_qk(psum_wide, "wide", 0, h) for h in range(HEADS)]
+            for h in range(HEADS):
+                vcopy(out=qk_cols[:, h, :, :], in_=turned[h][:])
+            sum_squares(q_rows[0], q2[0], range(UNITS))
+            square_k(0, 0)
+            split_q2(0)
+            add_k_squares(0, 0)
+            square_k(0, 1)
+            add_k_squares(0, 1)
+            xa, xb = new_x_pair(), new_x_pair()
+            turn_x(0, 0, xa, vcopy)
+            turn_x(0, 1, xa, vcopy)
+            turn_x(0, 2, xb, vcopy)
+            quantise_x_pair(0, 0, xa)
+            turn_x(0, 3, xb, vcopy)
+            quantise_x_pair(0, 1, xb)
+            turned = [turn_qk(psum_wide, "wide", 1, h) for h in range(HEADS)]
+            sum_squares(q_rows[1], q2[1], range(UNITS))
+            split_q2(1)
+            square_k(1, 0)
+            add_k_squares(1, 0)
+            square_k(1, 1)
+            add_k_squares(1, 1)
+            for h in range(HEADS):
+                scopy(out=qk_cols[:, HEADS + h, :, :], in_=turned[h][:])
             turn_q2(0)
-            prepare_qk(psum_wide, 1)
-            for pair in range(TILES // 2):
-                quantise_x_pair(1, pair)
-            turn_q2(1)
-            for s in range(GROUPS):
+            xa, xb = new_x_pair(), new_x_pair()
+            turn_x(1, 0, xa, vcopy)
+            turn_x(1, 1, xa, vcopy)
+            turn_x(1, 2, xb, vcopy)
+            quantise_x_pair(1, 0, xa)
+            turn_x(1, 3, xb, vcopy)
+            quantise_x_pair(1, 1, xb)
+            spread_bias(vcopy)
+            for h in range(HEADS):
+                if h == 2:
+                    turn_q2(1)
                 for t in range(TILES):
-                    logarithms(psum_wide, s, t)
-            project(1)
-
+                    logarithm(psum_wide, 0, h, t)
+                for j in (2 * h, 2 * h + 1):
+                    add_bias(0, j, project_chunk(0, j))
+            quantise_v(0, 0)
+            for i in reversed(range(TILES)):
+                floor(0, i)
+                mask(0, i)
+            quantise_v(0, 1)
+            for h in range(HEADS):
+                for t in range(TILES):
+                    logarithm(psum_wide, 1, h, t)
+                for j in ():
+                    if j // 1 == h:
+                        add_bias(1, j, project_chunk(1, j))
+        order = [(s, i) for s in range(GROUPS) for i in reversed(range(TILES))]
         with tc.psum_pool(name="out", bufs=4) as psum_out:
             previous = None
-            for s in range(GROUPS):
-                for i in reversed(range(TILES)):
-                    banks = attend(psum_out, s, i)
-                    if previous is not None:
-                        store(*previous)
-                    previous = (s, i, banks)
-            store(*previous)
+            for n, (s, i) in enumerate(order):
+                weigh(s, i)
+                if s == 0:
+                    floor(1, i)
+                    mask(1, i)
+                codes, scales = quantise_w(i)
+                chunks = [j for j in range(8) if j not in ()]
+                if n < 3:
+                    some = chunks[n * len(chunks) // 3 : (n + 1) * len(chunks) // 3]
+                    banks1 = [project_chunk(1, j) for j in some]
+                banks = attend(psum_out, s, codes, scales)
+                if n < 3:
+                    for j, bank in zip(some, banks1):
+                        add_bias(1, j, bank)
+                if n == 3:
+                    quantise_v(1, 0)
+                    quantise_v(1, 1)
+                if previous is not None:
+                    store(*previous)
+                previous = (s, i, banks, (vcopy, scopy))
+            store(previous[0], previous[1], previous[2], (vcopy, scopy))

@@ -39,6 +39,7 @@ def tile_networklayer_pb_kernel(tc, q_pos, k_pos, x_grp, Wv_words, Wv_scales, bv
         ident_bf = keep.tile([P, P], BF16)
         ident_f32 = keep.tile([P, P], F32)
         selector = keep.tile([P, UNITS], BF16)
+        causal_floor = keep.tile([P, P], F32)
         one = keep.tile([P, 1], F32)
         log_one = keep.tile([P, 1], F32)
         ones = keep.tile([P, P], BF16)
@@ -62,7 +63,7 @@ def tile_networklayer_pb_kernel(tc, q_pos, k_pos, x_grp, Wv_words, Wv_scales, bv
         q2_pieces = [keep.tile([P, P], BF16, name="q2_pieces%d" % s) for s in range(GROUPS)]
         q2_piece_rows = [keep.tile([P, P], BF16, name="q2_piece_rows%d" % s) for s in range(GROUPS)]
         log_d2 = [keep.tile([P, TILES, TILES, HEADS, P], F32, name="log_d2_%d" % s) for s in range(GROUPS)]
-        k_squares = keep.tile([P, UNITS, P], F32)
+        more_squares = keep.tile([P, UNITS, P], BF16)
         w_grouped = keep.tile([P, TILES, HEADS, P, PACK], BF16, align_bytes=64)
 
         nc.vector.memset(one[:], 1.0)
@@ -72,6 +73,16 @@ def tile_networklayer_pb_kernel(tc, q_pos, k_pos, x_grp, Wv_words, Wv_scales, bv
         make_identity(nc, ident_bf[:])
         nc.vector.memset(ones[:], 1.0)
         nc.vector.memset(bias_first[:].bitcast(I32), 0)
+        nc.vector.memset(causal_floor[:], LOG_FLOOR)
+        nc.gpsimd.affine_select(
+            out=causal_floor[:],
+            in_=causal_floor[:],
+            pattern=[[1, P]],
+            compare_op=ALU.is_ge,
+            fill=MASKED_LOG,
+            base=0,
+            channel_multiplier=-1,
+        )
         for s in range(GROUPS):
             nc.vector.memset(q2_pieces[s][:].bitcast(I32), 0)
         nc.vector.memset(w_grouped[:].rearrange("p i h b t -> p (i h b t)").bitcast(I32), 0)
@@ -79,30 +90,41 @@ def tile_networklayer_pb_kernel(tc, q_pos, k_pos, x_grp, Wv_words, Wv_scales, bv
         nc.vector.tensor_tensor(out=selector[:], in0=selector[:], in1=ident_bf[:, 2 * UNITS : 3 * UNITS], op=ALU.add)
         nc.vector.tensor_scalar(out=selector[:], in0=selector[:], scalar1=-0.5, scalar2=None, op0=ALU.mult)
 
-        def load_rows(rows, source):
-            nc.sync.dma_start(out=rows[:], in_=source.rearrange("h (i p) d -> p (h i) d", p=P))
+        def load_rows(rows, source, first, last):
+            nc.sync.dma_start(
+                out=rows[:, TILES * first : TILES * last, :],
+                in_=source[first:last].rearrange("h (i p) d -> p (h i) d", p=P),
+            )
 
-        def load_x(s, half):
-            tiles = slice(2 * half, 2 * half + 2)
-            nc.sync.dma_start(out=x_rows[s][:, tiles, :], in_=x_grp[s].rearrange("(t p) k -> p t k", p=P)[:, tiles, :])
+        def load_w(g, first, last):
+            nc.sync.dma_start(
+                out=w_words[:, g, first:last].bitcast(I32),
+                in_=Wv_words[g, :, first:last, :].rearrange("p n t -> p (n t)").bitcast(I32),
+            )
 
-        load_rows(q_rows[0], q_pos[0])
-        load_rows(k_rows[0], k_pos[0])
-        load_x(0, 0)
-        load_x(0, 1)
-        load_rows(q_rows[1], q_pos[1])
-        load_rows(k_rows[1], k_pos[1])
-        load_x(1, 0)
-        load_x(1, 1)
+        def load_x(s, first, last):
+            nc.sync.dma_start(
+                out=x_rows[s][:, first:last, :], in_=x_grp[s].rearrange("(t p) k -> p t k", p=P)[:, first:last, :]
+            )
+
+        load_rows(q_rows[0], q_pos[0], 0, 2)
+        load_rows(q_rows[0], q_pos[0], 2, 4)
+        load_x(0, 0, 2)
+        load_rows(k_rows[0], k_pos[0], 0, 2)
+        load_rows(k_rows[0], k_pos[0], 2, 4)
+        load_x(0, 2, 4)
+        load_rows(q_rows[1], q_pos[1], 0, HEADS)
+        load_rows(k_rows[1], k_pos[1], 0, HEADS)
         nc.sync.dma_start(out=bias_first[0:1, :], in_=bv.unsqueeze(0))
+        load_x(1, 0, 2)
         for quadrant in range(4):
             nc.sync.dma_start(
                 out=w_scales[32 * quadrant : 32 * quadrant + 4, :, :].bitcast(I32),
                 in_=Wv_scales[:, 4 * quadrant : 4 * quadrant + 4, :].rearrange("g r n -> r g n").bitcast(I32),
             )
-        for g in range(PASSES):
-            nc.sync.dma_start(out=w_words[:, g, :].bitcast(I32), in_=Wv_words[g].rearrange("p n t -> p (n t)").bitcast(I32))
-
+        load_w(0, 0, D_MODEL)
+        load_w(1, 0, D_MODEL)
+        load_x(1, 2, 4)
         def spread_bias(copy):
             for half in range(2):
                 cols = slice(4 * P * half, 4 * P * (half + 1))
@@ -167,31 +189,28 @@ def tile_networklayer_pb_kernel(tc, q_pos, k_pos, x_grp, Wv_words, Wv_scales, bv
         def turn_qk(pool, tag, s, h):
             turned = pool.tile([P, 2, TOKENS], BF16, tag=tag)
             for which, rows in enumerate((q_rows[s], k_rows[s])):
-                for i in range(TILES):
-                    nc.tensor.transpose(turned[:, which, P * i : P * (i + 1)], rows[:, TILES * h + i, :], ident_bf[:])
+                turn_rows(turned, which, rows, h)
             return turned
+
+        def turn_rows(turned, which, rows, h):
+            for i in range(TILES):
+                nc.tensor.transpose(turned[:, which, P * i : P * (i + 1)], rows[:, TILES * h + i, :], ident_bf[:])
 
         def sum_squares(rows, sums, units):
             for u in units:
                 nc.scalar.activation(out=squares[:, u, :], in_=rows[:, u, :], func=ACT.Square, accum_out=sums[:, u : u + 1])
 
-        def square_k(s, half):
-            for quarter in range(2):
-                some = slice(UNITS // 4 * (2 * half + quarter), UNITS // 4 * (2 * half + quarter + 1))
-                nc.gpsimd.tensor_tensor(
-                    out=k_squares[:, some, :], in0=k_rows[s][:, some, :], in1=k_rows[s][:, some, :], op=ALU.mult
+        def sum_squares_vector(rows, sums, units):
+            for u in units:
+                nc.vector.scalar_tensor_tensor(
+                    out=more_squares[:, u, :],
+                    in0=rows[:, u, :],
+                    scalar=1.0,
+                    in1=rows[:, u, :],
+                    op0=ALU.mult,
+                    op1=ALU.mult,
+                    accum_out=sums[:, u : u + 1],
                 )
-
-        def add_k_squares(s, half):
-            units = slice(UNITS // 2 * half, UNITS // 2 * (half + 1))
-            part = k_squares[:, units, :]
-            width = P // 2
-            while width > 1:
-                nc.gpsimd.tensor_tensor(
-                    out=part[:, :, 0:width], in0=part[:, :, 0:width], in1=part[:, :, width : 2 * width], op=ALU.add
-                )
-                width //= 2
-            nc.gpsimd.tensor_tensor(out=k2[s][:, units].unsqueeze(2), in0=part[:, :, 0:1], in1=part[:, :, 1:2], op=ALU.add)
 
         def split_q2(s):
             pieces = q2_pieces[s]
@@ -208,7 +227,7 @@ def tile_networklayer_pb_kernel(tc, q_pos, k_pos, x_grp, Wv_words, Wv_scales, bv
             nc.tensor.transpose(turned[:], q2_pieces[s][:], ident_bf[:])
             nc.vector.tensor_copy(out=q2_piece_rows[s][:], in_=turned[:])
 
-        def logarithm(psum_wide, s, h, t):
+        def distance(psum_wide, s, h, t):
             width = TOKENS - P * t
             q_cols = qk_cols[:, HEADS * s + h, 0, :]
             k_cols = qk_cols[:, HEADS * s + h, 1, :]
@@ -225,6 +244,10 @@ def tile_networklayer_pb_kernel(tc, q_pos, k_pos, x_grp, Wv_words, Wv_scales, bv
                     start=False,
                     stop=(i == TILES - 1),
                 )
+            return score
+
+        def logarithm(s, h, t, score):
+            width = TOKENS - P * t
             nc.scalar.activation(
                 out=log_d2[s][:, t:TILES, t, h, :],
                 in_=score[:, 0:width].rearrange("p (i b) -> p i b", b=P),
@@ -233,21 +256,14 @@ def tile_networklayer_pb_kernel(tc, q_pos, k_pos, x_grp, Wv_words, Wv_scales, bv
                 scale=-2.0,
             )
 
-        def floor(s, i):
-            live = log_d2[s][:, i, 0 : i + 1, :, :].rearrange("p t h b -> p (t h b)")
-            nc.vector.tensor_scalar(out=live, in0=live, scalar1=LOG_FLOOR, scalar2=None, op0=ALU.max)
-
-        def mask(s, i):
-            diagonal = log_d2[s][:, i, i, :, :]
-            nc.gpsimd.affine_select(
-                out=diagonal,
-                in_=diagonal,
-                pattern=[[0, HEADS], [1, P]],
-                compare_op=ALU.is_ge,
-                fill=MASKED_LOG,
-                base=0,
-                channel_multiplier=-1,
+        def floor_and_mask(s, t):
+            diagonal = log_d2[s][:, t, t, :, :]
+            nc.vector.tensor_tensor(
+                out=diagonal, in0=diagonal, in1=causal_floor[:].unsqueeze(1).to_broadcast([P, HEADS, P]), op=ALU.max
             )
+            if t < TILES - 1:
+                live = log_d2[s][:, t + 1 : TILES, t, :, :].rearrange("p i h b -> p i (h b)")
+                nc.vector.tensor_scalar(out=live, in0=live, scalar1=LOG_FLOOR, scalar2=None, op0=ALU.max)
 
         def weigh(s, i):
             nc.scalar.activation(
@@ -258,8 +274,8 @@ def tile_networklayer_pb_kernel(tc, q_pos, k_pos, x_grp, Wv_words, Wv_scales, bv
             )
 
         def quantise_w(i):
-            codes = ring.tile([P, HEADS * P], U32, align_bytes=64)
-            scales = ring.tile([P, HEADS * P], U8, align_bytes=64)
+            codes = ring.tile([P, HEADS * P], U32, align_bytes=64, bufs=5)
+            scales = ring.tile([P, HEADS * P], U8, align_bytes=64, bufs=5)
             nc.vector.quantize_mx(
                 out=codes[:].bitcast(FP8X4), scales=scales[:], in_=w_grouped[:, i].rearrange("p h b t -> p (h b t)")
             )
@@ -268,7 +284,7 @@ def tile_networklayer_pb_kernel(tc, q_pos, k_pos, x_grp, Wv_words, Wv_scales, bv
         def attend(psum_out, s, codes, scales):
             banks = []
             for pair in range(HEADS // 2):
-                bank = psum_out.tile([P, 2, D_HEAD], F32, tag="o_bank")
+                bank = psum_out.tile([P, 2, D_HEAD], F32, tag="wide")
                 for half in range(2):
                     h = 2 * pair + half
                     nc.tensor.matmul_mx(
@@ -291,32 +307,43 @@ def tile_networklayer_pb_kernel(tc, q_pos, k_pos, x_grp, Wv_words, Wv_scales, bv
 
         vcopy, scopy = nc.vector.tensor_copy, nc.scalar.copy
         with tc.psum_pool(name="wide", bufs=4) as psum_wide:
-            turned = [turn_qk(psum_wide, "wide", 0, h) for h in range(HEADS)]
-            for h in range(HEADS):
-                vcopy(out=qk_cols[:, h, :, :], in_=turned[h][:])
-            sum_squares(q_rows[0], q2[0], range(UNITS))
-            square_k(0, 0)
-            split_q2(0)
-            add_k_squares(0, 0)
-            square_k(0, 1)
-            add_k_squares(0, 1)
+            def scores(s, t):
+                for h in range(HEADS):
+                    logarithm(s, h, t, distance(psum_wide, s, h, t))
+
+            def project(s, j):
+                add_bias(s, j, project_chunk(s, j))
+
             xa, xb = new_x_pair(), new_x_pair()
+            turned = [psum_wide.tile([P, 2, TOKENS], BF16, tag="wide", name="turned%d" % h) for h in range(HEADS)]
+            for h in range(HEADS):
+                turn_rows(turned[h], 0, q_rows[0], h)
             turn_x(0, 0, xa, vcopy)
             turn_x(0, 1, xa, vcopy)
-            turn_x(0, 2, xb, vcopy)
+            sum_squares(q_rows[0], q2[0], range(UNITS))
+            split_q2(0)
+            for h in range(HEADS):
+                turn_rows(turned[h], 1, k_rows[0], h)
+            sum_squares(k_rows[0], k2[0], range(UNITS))
             quantise_x_pair(0, 0, xa)
+            for h in range(HEADS):
+                vcopy(out=qk_cols[:, h, :, :], in_=turned[h][:])
+            turn_q2(0)
+            turn_x(0, 2, xb, vcopy)
             turn_x(0, 3, xb, vcopy)
             quantise_x_pair(0, 1, xb)
-            turned = [turn_qk(psum_wide, "wide", 1, h) for h in range(HEADS)]
+            for t in range(TILES):
+                scores(0, t)
+                floor_and_mask(0, t)
+            spread_bias(vcopy)
             sum_squares(q_rows[1], q2[1], range(UNITS))
             split_q2(1)
-            square_k(1, 0)
-            add_k_squares(1, 0)
-            square_k(1, 1)
-            add_k_squares(1, 1)
+            turned = [turn_qk(psum_wide, "wide", 1, h) for h in range(HEADS)]
             for h in range(HEADS):
-                scopy(out=qk_cols[:, HEADS + h, :, :], in_=turned[h][:])
-            turn_q2(0)
+                (scopy if h < 2 else vcopy)(out=qk_cols[:, HEADS + h, :, :], in_=turned[h][:])
+            for i in reversed(range(TILES)):
+                weigh(0, i)
+            sum_squares(k_rows[1], k2[1], range(UNITS))
             xa, xb = new_x_pair(), new_x_pair()
             turn_x(1, 0, xa, vcopy)
             turn_x(1, 1, xa, vcopy)
@@ -324,46 +351,36 @@ def tile_networklayer_pb_kernel(tc, q_pos, k_pos, x_grp, Wv_words, Wv_scales, bv
             quantise_x_pair(1, 0, xa)
             turn_x(1, 3, xb, vcopy)
             quantise_x_pair(1, 1, xb)
-            spread_bias(vcopy)
-            for h in range(HEADS):
-                if h == 2:
-                    turn_q2(1)
-                for t in range(TILES):
-                    logarithm(psum_wide, 0, h, t)
-                for j in (2 * h, 2 * h + 1):
-                    add_bias(0, j, project_chunk(0, j))
-            quantise_v(0, 0)
-            for i in reversed(range(TILES)):
-                floor(0, i)
-                mask(0, i)
+            codes = []
+            for j in range(CHUNKS):
+                project(0, j)
+                if j % 2:
+                    codes.append(quantise_w(TILES - 1 - j // 2))
+                if j == 5:
+                    quantise_v(0, 0)
+            turn_q2(1)
             quantise_v(0, 1)
-            for h in range(HEADS):
-                for t in range(TILES):
-                    logarithm(psum_wide, 1, h, t)
-                for j in ():
-                    if j // 1 == h:
-                        add_bias(1, j, project_chunk(1, j))
-        order = [(s, i) for s in range(GROUPS) for i in reversed(range(TILES))]
-        with tc.psum_pool(name="out", bufs=4) as psum_out:
+            for j in range(2):
+                project(1, j)
+            for t in range(TILES):
+                scores(1, t)
+                project(1, 2 + t)
+                floor_and_mask(1, t)
+
+            quantise_v(1, 0)
+            for n in range(TILES):
+                banks = attend(psum_wide, 0, *codes[n])
+                for j in range(2 + TILES, CHUNKS):
+                    if (j - 2) % TILES == n:
+                        project(1, j)
+                store(0, TILES - 1 - n, banks, (vcopy, vcopy))
+            quantise_v(1, 1)
             previous = None
-            for n, (s, i) in enumerate(order):
-                weigh(s, i)
-                if s == 0:
-                    floor(1, i)
-                    mask(1, i)
+            for i in reversed(range(TILES)):
+                weigh(1, i)
                 codes, scales = quantise_w(i)
-                chunks = [j for j in range(8) if j not in ()]
-                if n < 3:
-                    some = chunks[n * len(chunks) // 3 : (n + 1) * len(chunks) // 3]
-                    banks1 = [project_chunk(1, j) for j in some]
-                banks = attend(psum_out, s, codes, scales)
-                if n < 3:
-                    for j, bank in zip(some, banks1):
-                        add_bias(1, j, bank)
-                if n == 3:
-                    quantise_v(1, 0)
-                    quantise_v(1, 1)
                 if previous is not None:
                     store(*previous)
-                previous = (s, i, banks, (vcopy, scopy))
-            store(previous[0], previous[1], previous[2], (vcopy, scopy))
+                banks = attend(psum_wide, 1, codes, scales)
+                previous = (1, i, banks, (vcopy, scopy if i == 0 else vcopy))
+            store(*previous)

@@ -56,14 +56,13 @@ def tile_networklayer_pb_kernel(tc, q_pos, k_pos, x_grp, Wv_words, Wv_scales, bv
         v_codes = keep.tile([P, GROUPS, D_MODEL], U32, align_bytes=64)
         v_scales = keep.tile([P, GROUPS, D_MODEL], U8, align_bytes=64)
         qk_cols = keep.tile([P, GROUPS * HEADS, 2, TOKENS], BF16)
-        squares = keep.tile([P, UNITS, P], BF16)
+        squares = keep.tile([P, P], BF16)
         q2 = [keep.tile([P, UNITS], F32, name="q2_%d" % s) for s in range(GROUPS)]
         k2 = [keep.tile([P, UNITS], F32, name="k2_%d" % s) for s in range(GROUPS)]
         q2_rest = [keep.tile([P, 2, UNITS], F32, name="q2_rest%d" % s) for s in range(GROUPS)]
         q2_pieces = [keep.tile([P, P], BF16, name="q2_pieces%d" % s) for s in range(GROUPS)]
         q2_piece_rows = [keep.tile([P, P], BF16, name="q2_piece_rows%d" % s) for s in range(GROUPS)]
         log_d2 = [keep.tile([P, TILES, TILES, HEADS, P], F32, name="log_d2_%d" % s) for s in range(GROUPS)]
-        more_squares = keep.tile([P, UNITS, P], BF16)
         w_grouped = keep.tile([P, TILES, HEADS, P, PACK], BF16, align_bytes=64)
 
         nc.vector.memset(one[:], 1.0)
@@ -109,9 +108,9 @@ def tile_networklayer_pb_kernel(tc, q_pos, k_pos, x_grp, Wv_words, Wv_scales, bv
 
         load_rows(q_rows[0], q_pos[0], 0, 2)
         load_rows(q_rows[0], q_pos[0], 2, 4)
-        load_x(0, 0, 2)
         load_rows(k_rows[0], k_pos[0], 0, 2)
         load_rows(k_rows[0], k_pos[0], 2, 4)
+        load_x(0, 0, 2)
         load_x(0, 2, 4)
         load_rows(q_rows[1], q_pos[1], 0, HEADS)
         load_rows(k_rows[1], k_pos[1], 0, HEADS)
@@ -126,11 +125,11 @@ def tile_networklayer_pb_kernel(tc, q_pos, k_pos, x_grp, Wv_words, Wv_scales, bv
         load_w(1, 0, D_MODEL)
         load_x(1, 2, 4)
         def spread_bias(copy):
+            bank = psum_work.tile([P, D_MODEL], BF16, tag="work")
             for half in range(2):
                 cols = slice(4 * P * half, 4 * P * (half + 1))
-                bank = psum_work.tile([P, 4 * P], F32, tag="work")
-                nc.tensor.matmul(out=bank[:], lhsT=ones[:], rhs=bias_first[:, cols], start=True, stop=True)
-                copy(out=bias_rows[:, cols], in_=bank[:])
+                nc.tensor.matmul(out=bank[:, cols], lhsT=ones[:], rhs=bias_first[:, cols], start=True, stop=True)
+            copy(out=bias_rows[:], in_=bank[:])
 
         def turn_x(s, n, x_grouped, copy):
             words = x_rows[s][:, n, :].bitcast(F32)
@@ -198,19 +197,7 @@ def tile_networklayer_pb_kernel(tc, q_pos, k_pos, x_grp, Wv_words, Wv_scales, bv
 
         def sum_squares(rows, sums, units):
             for u in units:
-                nc.scalar.activation(out=squares[:, u, :], in_=rows[:, u, :], func=ACT.Square, accum_out=sums[:, u : u + 1])
-
-        def sum_squares_vector(rows, sums, units):
-            for u in units:
-                nc.vector.scalar_tensor_tensor(
-                    out=more_squares[:, u, :],
-                    in0=rows[:, u, :],
-                    scalar=1.0,
-                    in1=rows[:, u, :],
-                    op0=ALU.mult,
-                    op1=ALU.mult,
-                    accum_out=sums[:, u : u + 1],
-                )
+                nc.scalar.activation(out=squares[:], in_=rows[:, u, :], func=ACT.Square, accum_out=sums[:, u : u + 1])
 
         def split_q2(s):
             pieces = q2_pieces[s]
@@ -281,10 +268,11 @@ def tile_networklayer_pb_kernel(tc, q_pos, k_pos, x_grp, Wv_words, Wv_scales, bv
             )
             return codes, scales
 
-        def attend(psum_out, s, codes, scales):
+        def attend(pools, s, codes, scales):
             banks = []
             for pair in range(HEADS // 2):
-                bank = psum_out.tile([P, 2, D_HEAD], F32, tag="wide")
+                pool, tag = pools[pair]
+                bank = pool.tile([P, 2, D_HEAD], F32, tag=tag)
                 for half in range(2):
                     h = 2 * pair + half
                     nc.tensor.matmul_mx(
@@ -299,10 +287,16 @@ def tile_networklayer_pb_kernel(tc, q_pos, k_pos, x_grp, Wv_words, Wv_scales, bv
                 banks.append(bank)
             return banks
 
-        def store(s, i, banks, copies):
+        def store_pair(s, i, pair, bank, copy):
+            half_result = ring.tile([P, 2 * D_HEAD], F32, bufs=8)
+            copy(out=half_result[:], in_=bank[:].rearrange("p e n -> p (e n)"))
+            cols = slice(2 * D_HEAD * pair, 2 * D_HEAD * (pair + 1))
+            nc.sync.dma_start(out=out[s, P * i : P * (i + 1), cols], in_=half_result[:])
+
+        def store(s, i, banks, copy):
             result = ring.tile([P, HEADS // 2, 2 * D_HEAD], F32)
             for pair, bank in enumerate(banks):
-                copies[pair](out=result[:, pair, :], in_=bank[:].rearrange("p e n -> p (e n)"))
+                copy(out=result[:, pair, :], in_=bank[:].rearrange("p e n -> p (e n)"))
             nc.sync.dma_start(out=out[s, P * i : P * (i + 1), :], in_=result[:].rearrange("p e n -> p (e n)"))
 
         vcopy, scopy = nc.vector.tensor_copy, nc.scalar.copy
@@ -318,23 +312,26 @@ def tile_networklayer_pb_kernel(tc, q_pos, k_pos, x_grp, Wv_words, Wv_scales, bv
             turned = [psum_wide.tile([P, 2, TOKENS], BF16, tag="wide", name="turned%d" % h) for h in range(HEADS)]
             for h in range(HEADS):
                 turn_rows(turned[h], 0, q_rows[0], h)
-            turn_x(0, 0, xa, vcopy)
-            turn_x(0, 1, xa, vcopy)
             sum_squares(q_rows[0], q2[0], range(UNITS))
             split_q2(0)
             for h in range(HEADS):
                 turn_rows(turned[h], 1, k_rows[0], h)
             sum_squares(k_rows[0], k2[0], range(UNITS))
-            quantise_x_pair(0, 0, xa)
             for h in range(HEADS):
                 vcopy(out=qk_cols[:, h, :, :], in_=turned[h][:])
             turn_q2(0)
-            turn_x(0, 2, xb, vcopy)
-            turn_x(0, 3, xb, vcopy)
-            quantise_x_pair(0, 1, xb)
             for t in range(TILES):
                 scores(0, t)
+                if t == 0:
+                    turn_x(0, 0, xa, vcopy)
+                    turn_x(0, 1, xa, vcopy)
+                    quantise_x_pair(0, 0, xa)
+                if t == 1:
+                    turn_x(0, 2, xb, vcopy)
+                    turn_x(0, 3, xb, vcopy)
+                    quantise_x_pair(0, 1, xb)
                 floor_and_mask(0, t)
+
             spread_bias(vcopy)
             sum_squares(q_rows[1], q2[1], range(UNITS))
             split_q2(1)
@@ -366,21 +363,22 @@ def tile_networklayer_pb_kernel(tc, q_pos, k_pos, x_grp, Wv_words, Wv_scales, bv
                 scores(1, t)
                 project(1, 2 + t)
                 floor_and_mask(1, t)
-
             quantise_v(1, 0)
-            for n in range(TILES):
-                banks = attend(psum_wide, 0, *codes[n])
+            for n in range(0, TILES):
+                banks = attend(((psum_wide, "wide"), (psum_wide, "wide")), 0, *codes[n])
                 for j in range(2 + TILES, CHUNKS):
-                    if (j - 2) % TILES == n:
+                    if j - 2 - TILES == n - 0:
                         project(1, j)
-                store(0, TILES - 1 - n, banks, (vcopy, vcopy))
+                store(0, TILES - 1 - n, banks, vcopy)
             quantise_v(1, 1)
-            previous = None
             for i in reversed(range(TILES)):
                 weigh(1, i)
+            last = []
+            for i in reversed(range(TILES)):
                 codes, scales = quantise_w(i)
-                if previous is not None:
-                    store(*previous)
-                banks = attend(psum_wide, 1, codes, scales)
-                previous = (1, i, banks, (vcopy, scopy if i == 0 else vcopy))
-            store(*previous)
+                if last:
+                    store_pair(1, i + 1, 0, last[-1][0], vcopy)
+                last.append(attend(((psum_work, "work"), (psum_wide, "wide")), 1, codes, scales))
+            store_pair(1, 0, 0, last[-1][0], vcopy)
+            for i in reversed(range(TILES)):
+                store_pair(1, i, 1, last[TILES - 1 - i][1], scopy)

@@ -56,13 +56,13 @@ def tile_networklayer_pb_kernel(tc, q_pos, k_pos, x_grp, Wv_words, Wv_scales, bv
         v_codes = keep.tile([P, GROUPS, D_MODEL], U32, align_bytes=64)
         v_scales = keep.tile([P, GROUPS, D_MODEL], U8, align_bytes=64)
         qk_cols = keep.tile([P, GROUPS * HEADS, 2, TOKENS], BF16)
-        squares = keep.tile([P, P], BF16)
+        squares = keep.tile([P, UNITS, P], BF16)
         q2 = [keep.tile([P, UNITS], F32, name="q2_%d" % s) for s in range(GROUPS)]
         k2 = [keep.tile([P, UNITS], F32, name="k2_%d" % s) for s in range(GROUPS)]
         q2_rest = [keep.tile([P, 2, UNITS], F32, name="q2_rest%d" % s) for s in range(GROUPS)]
         q2_pieces = [keep.tile([P, P], BF16, name="q2_pieces%d" % s) for s in range(GROUPS)]
         q2_piece_rows = [keep.tile([P, P], BF16, name="q2_piece_rows%d" % s) for s in range(GROUPS)]
-        log_d2 = [keep.tile([P, TILES, TILES, HEADS, P], F32, name="log_d2_%d" % s) for s in range(GROUPS)]
+        log_d2 = [keep.tile([P, 4 * TILES - 3, HEADS, P], F32, name="log_d2_%d" % s) for s in range(GROUPS)]
         w_grouped = keep.tile([P, TILES, HEADS, P, PACK], BF16, align_bytes=64)
 
         nc.vector.memset(one[:], 1.0)
@@ -197,7 +197,7 @@ def tile_networklayer_pb_kernel(tc, q_pos, k_pos, x_grp, Wv_words, Wv_scales, bv
 
         def sum_squares(rows, sums, units):
             for u in units:
-                nc.scalar.activation(out=squares[:], in_=rows[:, u, :], func=ACT.Square, accum_out=sums[:, u : u + 1])
+                nc.scalar.activation(out=squares[:, u, :], in_=rows[:, u, :], func=ACT.Square, accum_out=sums[:, u : u + 1])
 
         def split_q2(s):
             pieces = q2_pieces[s]
@@ -236,7 +236,7 @@ def tile_networklayer_pb_kernel(tc, q_pos, k_pos, x_grp, Wv_words, Wv_scales, bv
         def logarithm(s, h, t, score):
             width = TOKENS - P * t
             nc.scalar.activation(
-                out=log_d2[s][:, t:TILES, t, h, :],
+                out=log_d2[s][:, 4 * t : 3 * t + TILES, h, :],
                 in_=score[:, 0:width].rearrange("p (i b) -> p i b", b=P),
                 func=ACT.Ln,
                 bias=k2[s][:, TILES * h + t : TILES * h + t + 1],
@@ -244,18 +244,18 @@ def tile_networklayer_pb_kernel(tc, q_pos, k_pos, x_grp, Wv_words, Wv_scales, bv
             )
 
         def floor_and_mask(s, t):
-            diagonal = log_d2[s][:, t, t, :, :]
+            diagonal = log_d2[s][:, 4 * t, :, :]
             nc.vector.tensor_tensor(
                 out=diagonal, in0=diagonal, in1=causal_floor[:].unsqueeze(1).to_broadcast([P, HEADS, P]), op=ALU.max
             )
             if t < TILES - 1:
-                live = log_d2[s][:, t + 1 : TILES, t, :, :].rearrange("p i h b -> p i (h b)")
+                live = log_d2[s][:, 4 * t + 1 : 3 * t + TILES, :, :].rearrange("p i h b -> p (i h b)")
                 nc.vector.tensor_scalar(out=live, in0=live, scalar1=LOG_FLOOR, scalar2=None, op0=ALU.max)
 
         def weigh(s, i):
             nc.scalar.activation(
                 out=w_grouped[:, i, :, :, 0 : i + 1],
-                in_=log_d2[s][:, i, 0 : i + 1, :, :].rearrange("p t h b -> p h b t"),
+                in_=log_d2[s][:, i : 4 * i + 1 : 3, :, :].rearrange("p t h b -> p h b t"),
                 func=ACT.Sigmoid,
                 scale=-0.5,
             )
@@ -361,24 +361,26 @@ def tile_networklayer_pb_kernel(tc, q_pos, k_pos, x_grp, Wv_words, Wv_scales, bv
                 project(1, j)
             for t in range(TILES):
                 scores(1, t)
-                project(1, 2 + t)
+                for j in ((2,), (3,), (4, 5), (6, 7))[t]:
+                    project(1, j)
                 floor_and_mask(1, t)
-            quantise_v(1, 0)
-            for n in range(0, TILES):
-                banks = attend(((psum_wide, "wide"), (psum_wide, "wide")), 0, *codes[n])
-                for j in range(2 + TILES, CHUNKS):
-                    if j - 2 - TILES == n - 0:
-                        project(1, j)
-                store(0, TILES - 1 - n, banks, vcopy)
-            quantise_v(1, 1)
-            for i in reversed(range(TILES)):
+                if t == 2:
+                    quantise_v(1, 0)
+            order = (0, 3, 2, 1)
+            previous = None
+
+            for n, i in enumerate(order):
                 weigh(1, i)
-            last = []
-            for i in reversed(range(TILES)):
-                codes, scales = quantise_w(i)
-                if last:
-                    store_pair(1, i + 1, 0, last[-1][0], vcopy)
-                last.append(attend(((psum_work, "work"), (psum_wide, "wide")), 1, codes, scales))
-            store_pair(1, 0, 0, last[-1][0], vcopy)
-            for i in reversed(range(TILES)):
-                store_pair(1, i, 1, last[TILES - 1 - i][1], scopy)
+                if previous is not None:
+                    store_pair(1, order[n - 1], 1, previous[1], scopy)
+                banks = attend(((psum_wide, "wide"), (psum_wide, "wide")), 0, *codes[n])
+                if n == 0:
+                    quantise_v(1, 1)
+
+                w_codes = quantise_w(i)
+                store(0, TILES - 1 - n, banks, vcopy)
+                if previous is not None:
+                    store_pair(1, order[n - 1], 0, previous[0], vcopy)
+                previous = attend(((psum_work, "work"), (psum_work, "work")), 1, *w_codes)
+            store_pair(1, order[-1], 0, previous[0], vcopy)
+            store_pair(1, order[-1], 1, previous[1], scopy)

@@ -57,6 +57,7 @@ def tile_networklayer_pb_kernel(tc, q_pos, k_pos, x_grp, Wv_words, Wv_scales, bv
         v_scales = keep.tile([P, GROUPS, D_MODEL], U8, align_bytes=64)
         qk_cols = keep.tile([P, GROUPS * HEADS, 2, TOKENS], BF16)
         squares = keep.tile([P, UNITS, P], BF16)
+        squares_v = keep.tile([P, UNITS, P], BF16)
         q2 = [keep.tile([P, UNITS], F32, name="q2_%d" % s) for s in range(GROUPS)]
         k2 = [keep.tile([P, UNITS], F32, name="k2_%d" % s) for s in range(GROUPS)]
         q2_rest = [keep.tile([P, 2, UNITS], F32, name="q2_rest%d" % s) for s in range(GROUPS)]
@@ -110,9 +111,9 @@ def tile_networklayer_pb_kernel(tc, q_pos, k_pos, x_grp, Wv_words, Wv_scales, bv
         load_rows(q_rows[0], q_pos[0], 2, 4)
         load_rows(k_rows[0], k_pos[0], 0, 2)
         load_rows(k_rows[0], k_pos[0], 2, 4)
+        load_rows(q_rows[1], q_pos[1], 0, HEADS)
         load_x(0, 0, 2)
         load_x(0, 2, 4)
-        load_rows(q_rows[1], q_pos[1], 0, HEADS)
         load_rows(k_rows[1], k_pos[1], 0, HEADS)
         nc.sync.dma_start(out=bias_first[0:1, :], in_=bv.unsqueeze(0))
         load_x(1, 0, 2)
@@ -198,6 +199,18 @@ def tile_networklayer_pb_kernel(tc, q_pos, k_pos, x_grp, Wv_words, Wv_scales, bv
         def sum_squares(rows, sums, units):
             for u in units:
                 nc.scalar.activation(out=squares[:, u, :], in_=rows[:, u, :], func=ACT.Square, accum_out=sums[:, u : u + 1])
+
+        def sum_squares_vector(rows, sums, units):
+            for u in units:
+                nc.vector.scalar_tensor_tensor(
+                    out=squares_v[:, u, :],
+                    in0=rows[:, u, :],
+                    scalar=1.0,
+                    in1=rows[:, u, :],
+                    op0=ALU.mult,
+                    op1=ALU.mult,
+                    accum_out=sums[:, u : u + 1],
+                )
 
         def split_q2(s):
             pieces = q2_pieces[s]
@@ -312,14 +325,17 @@ def tile_networklayer_pb_kernel(tc, q_pos, k_pos, x_grp, Wv_words, Wv_scales, bv
             turned = [psum_wide.tile([P, 2, TOKENS], BF16, tag="wide", name="turned%d" % h) for h in range(HEADS)]
             for h in range(HEADS):
                 turn_rows(turned[h], 0, q_rows[0], h)
-            sum_squares(q_rows[0], q2[0], range(UNITS))
+            sum_squares(q_rows[0], q2[0], range(16))
+
             split_q2(0)
             for h in range(HEADS):
                 turn_rows(turned[h], 1, k_rows[0], h)
-            sum_squares(k_rows[0], k2[0], range(UNITS))
+            sum_squares(k_rows[0], k2[0], range(16))
             for h in range(HEADS):
                 vcopy(out=qk_cols[:, h, :, :], in_=turned[h][:])
             turn_q2(0)
+
+            sum_squares_vector(q_rows[1], q2[1], range(16))
             for t in range(TILES):
                 scores(0, t)
                 if t == 0:
@@ -333,14 +349,14 @@ def tile_networklayer_pb_kernel(tc, q_pos, k_pos, x_grp, Wv_words, Wv_scales, bv
                 floor_and_mask(0, t)
 
             spread_bias(vcopy)
-            sum_squares(q_rows[1], q2[1], range(UNITS))
             split_q2(1)
             turned = [turn_qk(psum_wide, "wide", 1, h) for h in range(HEADS)]
             for h in range(HEADS):
                 (scopy if h < 2 else vcopy)(out=qk_cols[:, HEADS + h, :, :], in_=turned[h][:])
+            sum_squares(k_rows[1], k2[1], range(UNITS))
             for i in reversed(range(TILES)):
                 weigh(0, i)
-            sum_squares(k_rows[1], k2[1], range(UNITS))
+
             xa, xb = new_x_pair(), new_x_pair()
             turn_x(1, 0, xa, vcopy)
             turn_x(1, 1, xa, vcopy)
@@ -349,18 +365,24 @@ def tile_networklayer_pb_kernel(tc, q_pos, k_pos, x_grp, Wv_words, Wv_scales, bv
             turn_x(1, 3, xb, vcopy)
             quantise_x_pair(1, 1, xb)
             codes = []
+            turn_q2(1)
             for j in range(CHUNKS):
                 project(0, j)
+                if j == 5:
+                    first_scores = [distance(psum_wide, 1, h, 0) for h in range(HEADS)]
                 if j % 2:
                     codes.append(quantise_w(TILES - 1 - j // 2))
                 if j == 5:
                     quantise_v(0, 0)
-            turn_q2(1)
             quantise_v(0, 1)
             for j in range(2):
                 project(1, j)
             for t in range(TILES):
-                scores(1, t)
+                if t == 0:
+                    for h in range(HEADS):
+                        logarithm(1, h, 0, first_scores[h])
+                else:
+                    scores(1, t)
                 for j in ((2,), (3,), (4, 5), (6, 7))[t]:
                     project(1, j)
                 floor_and_mask(1, t)

@@ -111,12 +111,11 @@ def tile_networklayer_pb_kernel(tc, q_pos, k_pos, x_grp, Wv_words, Wv_scales, bv
         load_rows(q_rows[0], q_pos[0], 2, 4)
         load_rows(k_rows[0], k_pos[0], 0, 2)
         load_rows(k_rows[0], k_pos[0], 2, 4)
+        nc.sync.dma_start(out=bias_first[0:1, :], in_=bv.unsqueeze(0))
         load_rows(q_rows[1], q_pos[1], 0, HEADS)
         load_x(0, 0, 2)
         load_x(0, 2, 4)
         load_rows(k_rows[1], k_pos[1], 0, HEADS)
-        nc.sync.dma_start(out=bias_first[0:1, :], in_=bv.unsqueeze(0))
-        load_x(1, 0, 2)
         for quadrant in range(4):
             nc.sync.dma_start(
                 out=w_scales[32 * quadrant : 32 * quadrant + 4, :, :].bitcast(I32),
@@ -124,7 +123,13 @@ def tile_networklayer_pb_kernel(tc, q_pos, k_pos, x_grp, Wv_words, Wv_scales, bv
             )
         load_w(0, 0, D_MODEL)
         load_w(1, 0, D_MODEL)
+        load_x(1, 0, 2)
         load_x(1, 2, 4)
+        def spread_mm(bank):
+            for half in range(2):
+                cols = slice(4 * P * half, 4 * P * (half + 1))
+                nc.tensor.matmul(out=bank[:, cols], lhsT=ones[:], rhs=bias_first[:, cols], start=True, stop=True)
+
         def spread_bias(copy):
             bank = psum_work.tile([P, D_MODEL], BF16, tag="work")
             for half in range(2):
@@ -333,7 +338,10 @@ def tile_networklayer_pb_kernel(tc, q_pos, k_pos, x_grp, Wv_words, Wv_scales, bv
             sum_squares(k_rows[0], k2[0], range(16))
             for h in range(HEADS):
                 vcopy(out=qk_cols[:, h, :, :], in_=turned[h][:])
+            bank = psum_work.tile([P, D_MODEL], BF16, tag="work")
+            spread_mm(bank)
             turn_q2(0)
+            vcopy(out=bias_rows[:], in_=bank[:])
 
             sum_squares_vector(q_rows[1], q2[1], range(16))
             for t in range(TILES):
@@ -348,7 +356,6 @@ def tile_networklayer_pb_kernel(tc, q_pos, k_pos, x_grp, Wv_words, Wv_scales, bv
                     quantise_x_pair(0, 1, xb)
                 floor_and_mask(0, t)
 
-            spread_bias(vcopy)
             split_q2(1)
             turned = [turn_qk(psum_wide, "wide", 1, h) for h in range(HEADS)]
             for h in range(HEADS):
@@ -357,6 +364,8 @@ def tile_networklayer_pb_kernel(tc, q_pos, k_pos, x_grp, Wv_words, Wv_scales, bv
             for i in reversed(range(TILES)):
                 weigh(0, i)
 
+            for j in range(2):
+                project(0, j)
             xa, xb = new_x_pair(), new_x_pair()
             turn_x(1, 0, xa, vcopy)
             turn_x(1, 1, xa, vcopy)
@@ -367,7 +376,8 @@ def tile_networklayer_pb_kernel(tc, q_pos, k_pos, x_grp, Wv_words, Wv_scales, bv
             codes = []
             turn_q2(1)
             for j in range(CHUNKS):
-                project(0, j)
+                if j >= 2:
+                    project(0, j)
                 if j == 5:
                     first_scores = [distance(psum_wide, 1, h, 0) for h in range(HEADS)]
                 if j % 2:
@@ -390,7 +400,6 @@ def tile_networklayer_pb_kernel(tc, q_pos, k_pos, x_grp, Wv_words, Wv_scales, bv
                     quantise_v(1, 0)
             order = (0, 3, 2, 1)
             previous = None
-
             for n, i in enumerate(order):
                 weigh(1, i)
                 if previous is not None:
@@ -398,9 +407,12 @@ def tile_networklayer_pb_kernel(tc, q_pos, k_pos, x_grp, Wv_words, Wv_scales, bv
                 banks = attend(((psum_wide, "wide"), (psum_wide, "wide")), 0, *codes[n])
                 if n == 0:
                     quantise_v(1, 1)
-
                 w_codes = quantise_w(i)
-                store(0, TILES - 1 - n, banks, vcopy)
+                if n < 3:
+                    store(0, TILES - 1 - n, banks, vcopy)
+                else:
+                    store_pair(0, TILES - 1 - n, 0, banks[0], vcopy)
+                    store_pair(0, TILES - 1 - n, 1, banks[1], scopy)
                 if previous is not None:
                     store_pair(1, order[n - 1], 0, previous[0], vcopy)
                 previous = attend(((psum_work, "work"), (psum_work, "work")), 1, *w_codes)

import math

import concourse.mybir as mybir
from concourse.masks import make_identity

FLOPS = 2 * 1024 * 1024 * 1024 + 8 * 2 * 512 * 512 * (128 + 256)

F32 = mybir.dt.float32
BF16 = mybir.dt.bfloat16
I32 = mybir.dt.int32
U32 = mybir.dt.uint32
U8 = mybir.dt.uint8
FP8X4 = mybir.dt.float8_e4m3fn_x4
ACT = mybir.ActivationFunctionType
ALU = mybir.AluOpType

P = 128
PACK = 4
GROUPS = 2
HEADS = 4
TOKENS = 512
TILES = TOKENS // P
D_MODEL = 1024
PASSES = D_MODEL // (P * PACK)
D_HEAD = D_MODEL // HEADS
CHUNKS = D_MODEL // P
UNITS = HEADS * TILES
PIECES = 3
D2_FLOOR = 1e-12
LOG_FLOOR = math.log(D2_FLOOR)
MASKED_LOG = 1e30


def tile_networklayer_pb_kernel(tc, q_pos, k_pos, x_grp, Wv_words, Wv_scales, bv, out):
    nc = tc.nc
    with tc.tile_pool(name="keep", bufs=1) as keep, tc.tile_pool(name="ring", bufs=3) as ring, tc.psum_pool(
        name="work", bufs=4
    ) as psum_work, tc.manual_schedule():
        ident_bf = keep.tile([P, P], BF16)
        ident_f32 = keep.tile([P, P], F32)
        selector = keep.tile([P, UNITS], BF16)
        causal_floor = keep.tile([P, P], F32)
        one = keep.tile([P, 1], F32)
        log_one = keep.tile([P, 1], F32)
        ones = keep.tile([P, P], BF16)
        bias_first = keep.tile([P, D_MODEL], BF16)
        bias_rows = keep.tile([P, D_MODEL], BF16)
        q_rows = [keep.tile([P, UNITS, P], BF16, name="q_rows%d" % s) for s in range(GROUPS)]
        k_rows = [keep.tile([P, UNITS, P], BF16, name="k_rows%d" % s) for s in range(GROUPS)]
        x_rows = [keep.tile([P, TILES, D_MODEL], BF16, name="x_rows%d" % s) for s in range(GROUPS)]
        w_words = keep.tile([P, PASSES, D_MODEL], U32, align_bytes=64)
        w_scales = keep.tile([P, PASSES, D_MODEL], U8, align_bytes=64)
        x_codes = keep.tile([P, GROUPS * TILES, PASSES * P], U32, align_bytes=64)
        x_scales = keep.tile([P, GROUPS * TILES, PASSES * P], U8, align_bytes=64)
        v_grouped = [keep.tile([P, D_MODEL, PACK], BF16, name="v_grouped%d" % s, align_bytes=64) for s in range(GROUPS)]
        v_codes = keep.tile([P, GROUPS, D_MODEL], U32, align_bytes=64)
        v_scales = keep.tile([P, GROUPS, D_MODEL], U8, align_bytes=64)
        qk_cols = keep.tile([P, GROUPS * HEADS, 2, TOKENS], BF16)
        squares = keep.tile([P, UNITS, P], BF16)
        squares_v = keep.tile([P, UNITS, P], BF16)
        q2 = [keep.tile([P, UNITS], F32, name="q2_%d" % s) for s in range(GROUPS)]
        k2 = [keep.tile([P, UNITS], F32, name="k2_%d" % s) for s in range(GROUPS)]
        q2_rest = [keep.tile([P, 2, UNITS], F32, name="q2_rest%d" % s) for s in range(GROUPS)]
        q2_pieces = [keep.tile([P, P], BF16, name="q2_pieces%d" % s) for s in range(GROUPS)]
        q2_piece_rows = [keep.tile([P, P], BF16, name="q2_piece_rows%d" % s) for s in range(GROUPS)]
        log_d2 = [keep.tile([P, 4 * TILES - 3, HEADS, P], F32, name="log_d2_%d" % s) for s in range(GROUPS)]
        w_grouped = keep.tile([P, TILES, HEADS, P, PACK], BF16, align_bytes=64)

        nc.vector.memset(one[:], 1.0)
        nc.scalar.activation(out=log_one[:], in_=one[:], func=ACT.Ln)
        nc.vector.memset(w_scales[:].rearrange("p g n -> p (g n)").bitcast(I32), 0)
        make_identity(nc, ident_f32[:])
        make_identity(nc, ident_bf[:])
        nc.vector.memset(ones[:], 1.0)
        nc.vector.memset(bias_first[:].bitcast(I32), 0)
        nc.vector.memset(causal_floor[:], LOG_FLOOR)
        nc.gpsimd.affine_select(
            out=causal_floor[:],
            in_=causal_floor[:],
            pattern=[[1, P]],
            compare_op=ALU.is_ge,
            fill=MASKED_LOG,
            base=0,
            channel_multiplier=-1,
        )
        for s in range(GROUPS):
            nc.vector.memset(q2_pieces[s][:].bitcast(I32), 0)
        nc.vector.memset(w_grouped[:].rearrange("p i h b t -> p (i h b t)").bitcast(I32), 0)
        nc.vector.tensor_tensor(out=selector[:], in0=ident_bf[:, 0:UNITS], in1=ident_bf[:, UNITS : 2 * UNITS], op=ALU.add)
        nc.vector.tensor_tensor(out=selector[:], in0=selector[:], in1=ident_bf[:, 2 * UNITS : 3 * UNITS], op=ALU.add)
        nc.vector.tensor_scalar(out=selector[:], in0=selector[:], scalar1=-0.5, scalar2=None, op0=ALU.mult)

        def load_rows(rows, source, first, last):
            nc.sync.dma_start(
                out=rows[:, TILES * first : TILES * last, :],
                in_=source[first:last].rearrange("h (i p) d -> p (h i) d", p=P),
            )

        def load_w(g, first, last):
            nc.sync.dma_start(
                out=w_words[:, g, first:last].bitcast(I32),
                in_=Wv_words[g, :, first:last, :].rearrange("p n t -> p (n t)").bitcast(I32),
            )

        def load_x(s, first, last):
            nc.sync.dma_start(
                out=x_rows[s][:, first:last, :], in_=x_grp[s].rearrange("(t p) k -> p t k", p=P)[:, first:last, :]
            )

        load_rows(q_rows[0], q_pos[0], 0, 2)
        load_rows(q_rows[0], q_pos[0], 2, 4)
        load_rows(k_rows[0], k_pos[0], 0, 2)
        load_rows(k_rows[0], k_pos[0], 2, 4)
        nc.sync.dma_start(out=bias_first[0:1, :], in_=bv.unsqueeze(0))
        load_rows(q_rows[1], q_pos[1], 0, HEADS)
        load_x(0, 0, 2)
        load_x(0, 2, 4)
        load_rows(k_rows[1], k_pos[1], 0, HEADS)
        for quadrant in range(4):
            nc.sync.dma_start(
                out=w_scales[32 * quadrant : 32 * quadrant + 4, :, :].bitcast(I32),
                in_=Wv_scales[:, 4 * quadrant : 4 * quadrant + 4, :].rearrange("g r n -> r g n").bitcast(I32),
            )
        load_w(0, 0, D_MODEL)
        load_w(1, 0, D_MODEL)
        load_x(1, 0, 2)
        load_x(1, 2, 4)
        def spread_mm(bank):
            for half in range(2):
                cols = slice(4 * P * half, 4 * P * (half + 1))
                nc.tensor.matmul(out=bank[:, cols], lhsT=ones[:], rhs=bias_first[:, cols], start=True, stop=True)

        def spread_bias(copy):
            bank = psum_work.tile([P, D_MODEL], BF16, tag="work")
            for half in range(2):
                cols = slice(4 * P * half, 4 * P * (half + 1))
                nc.tensor.matmul(out=bank[:, cols], lhsT=ones[:], rhs=bias_first[:, cols], start=True, stop=True)
            copy(out=bias_rows[:], in_=bank[:])

        def turn_x(s, n, x_grouped, copy):
            words = x_rows[s][:, n, :].bitcast(F32)
            turned = psum_work.tile([P, PASSES, 2, P], F32, tag="work")
            for g in range(PASSES):
                for u in range(2):
                    nc.tensor.transpose(turned[:, g, u, :], words[:, 256 * g + u : 256 * (g + 1) : 2], ident_f32[:])
            copy(out=x_grouped[:, n % 2].bitcast(F32), in_=turned[:].rearrange("p g u m -> p g m u"))

        def new_x_pair():
            x_grouped = ring.tile([P, 2, PASSES, P, PACK], BF16, align_bytes=64)
            return x_grouped

        def quantise_x_pair(s, pair, x_grouped):
            tiles = slice(TILES * s + 2 * pair, TILES * s + 2 * pair + 2)
            nc.vector.quantize_mx(
                out=x_codes[:, tiles, :].rearrange("p n w -> p (n w)").bitcast(FP8X4),
                scales=x_scales[:, tiles, :].rearrange("p n w -> p (n w)"),
                in_=x_grouped[:].rearrange("p n g m j -> p (n g m j)"),
            )

        def project_chunk(s, j):
            cols = slice(P * j, P * (j + 1))
            bank = psum_work.tile([P, TILES, P], F32, tag="work")
            for t in range(TILES):
                for g in range(PASSES):
                    tokens = slice(P * g, P * (g + 1))
                    nc.tensor.matmul_mx(
                        out=bank[:, t, :],
                        lhsT=x_codes[:, TILES * s + t, tokens].bitcast(FP8X4),
                        lhsT_scale=x_scales[:, TILES * s + t, tokens],
                        rhs=w_words[:, g, cols].bitcast(FP8X4),
                        rhs_scale=w_scales[:, g, cols],
                        start=(g == 0),
                        stop=(g == PASSES - 1),
                    )
            return bank

        def add_bias(s, j, bank):
            cols = slice(P * j, P * (j + 1))
            nc.vector.tensor_tensor(
                out=v_grouped[s][:, cols, :],
                in0=bank[:].rearrange("p t n -> p n t"),
                in1=bias_rows[:, cols].unsqueeze(2).to_broadcast([P, P, PACK]),
                op=ALU.add,
            )

        def quantise_v(s, half):
            cols = slice(2 * D_HEAD * half, 2 * D_HEAD * (half + 1))
            nc.vector.quantize_mx(
                out=v_codes[:, s, cols].bitcast(FP8X4),
                scales=v_scales[:, s, cols],
                in_=v_grouped[s][:, cols, :].rearrange("p n t -> p (n t)"),
            )

        def turn_qk(pool, tag, s, h):
            turned = pool.tile([P, 2, TOKENS], BF16, tag=tag)
            for which, rows in enumerate((q_rows[s], k_rows[s])):
                turn_rows(turned, which, rows, h)
            return turned

        def turn_rows(turned, which, rows, h):
            for i in range(TILES):
                nc.tensor.transpose(turned[:, which, P * i : P * (i + 1)], rows[:, TILES * h + i, :], ident_bf[:])

        def sum_squares(rows, sums, units):
            for u in units:
                nc.scalar.activation(out=squares[:, u, :], in_=rows[:, u, :], func=ACT.Square, accum_out=sums[:, u : u + 1])

        def sum_squares_vector(rows, sums, units):
            for u in units:
                nc.vector.scalar_tensor_tensor(
                    out=squares_v[:, u, :],
                    in0=rows[:, u, :],
                    scalar=1.0,
                    in1=rows[:, u, :],
                    op0=ALU.mult,
                    op1=ALU.mult,
                    accum_out=sums[:, u : u + 1],
                )

        def split_q2(s):
            pieces = q2_pieces[s]
            rest = q2[s][:]
            for n in range(PIECES):
                piece = pieces[:, UNITS * n : UNITS * (n + 1)]
                nc.gpsimd.tensor_copy(out=piece, in_=rest)
                if n < PIECES - 1:
                    nc.gpsimd.tensor_tensor(out=q2_rest[s][:, n, :], in0=rest, in1=piece, op=ALU.subtract)
                    rest = q2_rest[s][:, n, :]

        def turn_q2(s):
            turned = psum_work.tile([P, P], BF16, tag="work")
            nc.tensor.transpose(turned[:], q2_pieces[s][:], ident_bf[:])
            nc.vector.tensor_copy(out=q2_piece_rows[s][:], in_=turned[:])

        def distance(psum_wide, s, h, t):
            width = TOKENS - P * t
            q_cols = qk_cols[:, HEADS * s + h, 0, :]
            k_cols = qk_cols[:, HEADS * s + h, 1, :]
            score = psum_wide.tile([P, TOKENS], F32, tag="wide")
            nc.tensor.matmul(
                out=score[:, 0:width], lhsT=k_cols[:, P * t : P * (t + 1)], rhs=q_cols[:, P * t : TOKENS], start=True, stop=False
            )
            for i in range(t, TILES):
                u = TILES * h + i
                nc.tensor.matmul(
                    out=score[:, P * (i - t) : P * (i - t + 1)],
                    lhsT=selector[:, u : u + 1].to_broadcast([P, P]),
                    rhs=q2_piece_rows[s][:],
                    start=False,
                    stop=(i == TILES - 1),
                )
            return score

        def logarithm(s, h, t, score):
            width = TOKENS - P * t
            nc.scalar.activation(
                out=log_d2[s][:, 4 * t : 3 * t + TILES, h, :],
                in_=score[:, 0:width].rearrange("p (i b) -> p i b", b=P),
                func=ACT.Ln,
                bias=k2[s][:, TILES * h + t : TILES * h + t + 1],
                scale=-2.0,
            )

        def floor_and_mask(s, t):
            diagonal = log_d2[s][:, 4 * t, :, :]
            nc.vector.tensor_tensor(
                out=diagonal, in0=diagonal, in1=causal_floor[:].unsqueeze(1).to_broadcast([P, HEADS, P]), op=ALU.max
            )
            if t < TILES - 1:
                live = log_d2[s][:, 4 * t + 1 : 3 * t + TILES, :, :].rearrange("p i h b -> p (i h b)")
                nc.vector.tensor_scalar(out=live, in0=live, scalar1=LOG_FLOOR, scalar2=None, op0=ALU.max)

        def weigh(s, i):
            nc.scalar.activation(
                out=w_grouped[:, i, :, :, 0 : i + 1],
                in_=log_d2[s][:, i : 4 * i + 1 : 3, :, :].rearrange("p t h b -> p h b t"),
                func=ACT.Sigmoid,
                scale=-0.5,
            )

        def quantise_w(i):
            codes = ring.tile([P, HEADS * P], U32, align_bytes=64, bufs=5)
            scales = ring.tile([P, HEADS * P], U8, align_bytes=64, bufs=5)
            nc.vector.quantize_mx(
                out=codes[:].bitcast(FP8X4), scales=scales[:], in_=w_grouped[:, i].rearrange("p h b t -> p (h b t)")
            )
            return codes, scales

        def attend(pools, s, codes, scales):
            banks = []
            for pair in range(HEADS // 2):
                pool, tag = pools[pair]
                bank = pool.tile([P, 2, D_HEAD], F32, tag=tag)
                for half in range(2):
                    h = 2 * pair + half
                    nc.tensor.matmul_mx(
                        out=bank[:, half, :],
                        lhsT=codes[:, P * h : P * (h + 1)].bitcast(FP8X4),
                        lhsT_scale=scales[:, P * h : P * (h + 1)],
                        rhs=v_codes[:, s, D_HEAD * h : D_HEAD * (h + 1)].bitcast(FP8X4),
                        rhs_scale=v_scales[:, s, D_HEAD * h : D_HEAD * (h + 1)],
                        start=True,
                        stop=True,
                    )
                banks.append(bank)
            return banks

        def store_pair(s, i, pair, bank, copy):
            half_result = ring.tile([P, 2 * D_HEAD], F32, bufs=8)
            copy(out=half_result[:], in_=bank[:].rearrange("p e n -> p (e n)"))
            cols = slice(2 * D_HEAD * pair, 2 * D_HEAD * (pair + 1))
            nc.sync.dma_start(out=out[s, P * i : P * (i + 1), cols], in_=half_result[:])

        def store(s, i, banks, copy):
            result = ring.tile([P, HEADS // 2, 2 * D_HEAD], F32)
            for pair, bank in enumerate(banks):
                copy(out=result[:, pair, :], in_=bank[:].rearrange("p e n -> p (e n)"))
            nc.sync.dma_start(out=out[s, P * i : P * (i + 1), :], in_=result[:].rearrange("p e n -> p (e n)"))

        vcopy, scopy = nc.vector.tensor_copy, nc.scalar.copy
        with tc.psum_pool(name="wide", bufs=4) as psum_wide:
            def scores(s, t):
                for h in range(HEADS):
                    logarithm(s, h, t, distance(psum_wide, s, h, t))

            def project(s, j):
                add_bias(s, j, project_chunk(s, j))

            xa, xb = new_x_pair(), new_x_pair()
            turned = [psum_wide.tile([P, 2, TOKENS], BF16, tag="wide", name="turned%d" % h) for h in range(HEADS)]
            for h in range(HEADS):
                turn_rows(turned[h], 0, q_rows[0], h)
            sum_squares(q_rows[0], q2[0], range(16))

            split_q2(0)
            for h in range(HEADS):
                turn_rows(turned[h], 1, k_rows[0], h)
            sum_squares(k_rows[0], k2[0], range(16))
            for h in range(HEADS):
                vcopy(out=qk_cols[:, h, :, :], in_=turned[h][:])
            bank = psum_work.tile([P, D_MODEL], BF16, tag="work")
            spread_mm(bank)
            turn_q2(0)
            vcopy(out=bias_rows[:], in_=bank[:])

            sum_squares_vector(q_rows[1], q2[1], range(16))
            for t in range(TILES):
                scores(0, t)
                if t == 0:
                    turn_x(0, 0, xa, vcopy)
                    turn_x(0, 1, xa, vcopy)
                    quantise_x_pair(0, 0, xa)
                if t == 1:
                    turn_x(0, 2, xb, vcopy)
                    turn_x(0, 3, xb, vcopy)
                    quantise_x_pair(0, 1, xb)
                floor_and_mask(0, t)

            split_q2(1)
            turned = [turn_qk(psum_wide, "wide", 1, h) for h in range(HEADS)]
            for h in range(HEADS):
                (scopy if h < 2 else vcopy)(out=qk_cols[:, HEADS + h, :, :], in_=turned[h][:])
            sum_squares(k_rows[1], k2[1], range(UNITS))
            for i in reversed(range(TILES)):
                weigh(0, i)

            for j in range(2):
                project(0, j)
            xa, xb = new_x_pair(), new_x_pair()
            turn_x(1, 0, xa, vcopy)
            turn_x(1, 1, xa, vcopy)
            turn_x(1, 2, xb, vcopy)
            quantise_x_pair(1, 0, xa)
            turn_x(1, 3, xb, vcopy)
            quantise_x_pair(1, 1, xb)
            codes = []
            turn_q2(1)
            for j in range(CHUNKS):
                if j >= 2:
                    project(0, j)
                if j == 5:
                    first_scores = [distance(psum_wide, 1, h, 0) for h in range(HEADS)]
                if j % 2:
                    codes.append(quantise_w(TILES - 1 - j // 2))
                if j == 5:
                    quantise_v(0, 0)
            quantise_v(0, 1)
            for j in range(2):
                project(1, j)
            for t in range(TILES):
                if t == 0:
                    for h in range(HEADS):
                        logarithm(1, h, 0, first_scores[h])
                else:
                    scores(1, t)
                for j in ((2,), (3,), (4, 5), (6, 7))[t]:
                    project(1, j)
                floor_and_mask(1, t)
                if t == 2:
                    quantise_v(1, 0)
            order = (0, 3, 2, 1)
            previous = None
            for n, i in enumerate(order):
                weigh(1, i)
                if previous is not None:
                    store_pair(1, order[n - 1], 1, previous[1], scopy)
                banks = attend(((psum_wide, "wide"), (psum_wide, "wide")), 0, *codes[n])
                if n == 0:
                    quantise_v(1, 1)
                w_codes = quantise_w(i)
                if n < 3:
                    store(0, TILES - 1 - n, banks, vcopy)
                else:
                    store_pair(0, TILES - 1 - n, 0, banks[0], vcopy)
                    store_pair(0, TILES - 1 - n, 1, banks[1], scopy)
                if previous is not None:
                    store_pair(1, order[n - 1], 0, previous[0], vcopy)
                previous = attend(((psum_work, "work"), (psum_work, "work")), 1, *w_codes)
            store_pair(1, order[-1], 0, previous[0], vcopy)
            store_pair(1, order[-1], 1, previous[1], scopy)
